import numpy as np
import ml_dtypes


def mxq(x, axis, fmt="e4m3"):
    dtype, down = {"e4m3": (ml_dtypes.float8_e4m3fn, 7), "e5m2": (ml_dtypes.float8_e5m2, 14)}[fmt]
    v = np.moveaxis(np.asarray(x, np.float32).astype(ml_dtypes.bfloat16).astype(np.float64), axis, -1)
    blocks = v.reshape(v.shape[:-1] + (-1, 32))
    amax = np.abs(blocks).max(-1, keepdims=True)
    byte = np.maximum(np.where(amax > 0, np.frexp(amax)[1] - 1 + 127, 0) - down, 1)
    scale = np.exp2(byte - 127.0)
    codes = (blocks / scale).astype(np.float32).astype(dtype).astype(np.float64)
    return np.moveaxis((codes * scale).reshape(v.shape), -1, axis)


WIDE = False


def mx_kscale(k):
    if not WIDE:
        return np.ones(k)
    levels = np.array([10, -10, 5, -5, 0])
    a = np.random.permutation(np.resize(levels, k // 512 * 4)).reshape(k // 512, 4)
    idx = np.arange(k)
    return np.exp2(a[idx // 512, idx % 128 // 32])


BF16 = ml_dtypes.bfloat16


def bf(x):
    return np.asarray(x, np.float32).astype(BF16)


def f64(x):
    return np.asarray(x).astype(np.float64)


N, L, A, D = 64, 128, 16, 32
KP, KQ = A * D, D * D


def setup_inputs():
    u = mx_kscale(KP).reshape(A, D)[:, 0].copy()
    u[-1] = 1.0
    t = mx_kscale(KQ).reshape(D, D)[:, 0].copy()
    t[-1] = 1.0
    return {"layer1": bf(np.random.standard_normal((N, L, A - 1)) * u[:-1]),
            "layer2": bf(np.random.standard_normal((N, L, D - 1)) * 0.5 / t[:-1]),
            "layer3": bf(np.random.standard_normal((N, L, D - 1))),
            "h1": bf(np.random.standard_normal((N, L, D))),
            "h2": bf(np.random.standard_normal((N, L, D)) * 0.5),
            "h3": bf(np.random.standard_normal((N, L, D))),
            "W": bf(np.random.standard_normal((A, D, D, D)) * 0.4 / np.sqrt(KP) / u[:, None, None, None] * t[None, :, None, None])}


def reference(layer1, layer2, layer3, h1, h2, h3, W):
    n, l = layer1.shape[:2]
    ones = np.ones((n, l, 1))
    l1 = np.concatenate([f64(layer1), ones], axis=-1)
    l2 = np.concatenate([f64(layer2), ones], axis=-1)
    p = (l1[..., :, None] * f64(h1)[..., None, :]).reshape(n, l, KP)
    w = f64(W).transpose(0, 2, 1, 3).reshape(KP, KQ)
    q = mxq(p, 2, "e4m3") @ mxq(w, 0, "e4m3")
    r = (l2[..., :, None] * f64(h2)[..., None, :]).reshape(n, l, KQ)
    return mxq(q, 2, "e4m3") @ mxq(r, 2, "e4m3").transpose(0, 2, 1)

@@ -1,0 +1,252 @@
+from contextlib import ExitStack
+
+import concourse.mybir as mybir
+from concourse.masks import make_identity
+
+F32 = mybir.dt.float32
+BF16 = mybir.dt.bfloat16
+U8 = mybir.dt.uint8
+U32 = mybir.dt.uint32
+I32 = mybir.dt.int32
+FP8X4 = mybir.dt.float8_e4m3fn_x4
+MULT = mybir.AluOpType.mult
+
+P = 128
+NB = 64
+CB = 4
+NCH = NB // CB
+GB = 16
+NG = NB // GB
+NU = 4 * NCH
+FLOPS = 2 * 8192 * 512 * 1024 + 2 * 64 * 128 * 128 * 1024
+
+LS_WORDS = 48 * GB * 128
+LS_BASE = NB * P * P - NG * LS_WORDS
+
+
+def tile_qriaffine_t_kernel(tc, layer1, layer2, layer3, h1, h2, h3, W, out):
+    nc = tc.nc
+    with ExitStack() as ctx:
+        const = ctx.enter_context(tc.tile_pool(name="const", bufs=1))
+        inp = ctx.enter_context(tc.tile_pool(name="inp", bufs=1))
+        lpp = ctx.enter_context(tc.tile_pool(name="lpp", bufs=2))
+        yp = ctx.enter_context(tc.tile_pool(name="yp", bufs=2))
+        lrp = ctx.enter_context(tc.tile_pool(name="lrp", bufs=3))
+        work = ctx.enter_context(tc.tile_pool(name="work", bufs=2))
+        outp = ctx.enter_context(tc.tile_pool(name="outp", bufs=3))
+        ps_h = ctx.enter_context(tc.psum_pool(name="ps_h", bufs=3))
+        ps_q = ctx.enter_context(tc.psum_pool(name="ps_q", bufs=3))
+        ps_o = ctx.enter_context(tc.psum_pool(name="ps_o", bufs=1))
+        ps_l = ctx.enter_context(tc.psum_pool(name="ps_l", bufs=1))
+        ctx.enter_context(tc.manual_schedule())
+
+        ident_b = const.tile([P, P], BF16, name="ident_b")
+        make_identity(nc, ident_b[:])
+        ident_f = const.tile([P, P], F32, name="ident_f")
+        make_identity(nc, ident_f[:])
+
+        lv2 = layer2.rearrange("n j b -> j n b")
+        lv1 = layer1.rearrange("n j b -> j n b")
+        hv = [
+            h1.rearrange("n (a j) (u w) -> (j u) (n a) w", a=2, u=2),
+            h2.rearrange("n (a j) (u w) -> (j u) (n a) w", a=2, u=2),
+        ]
+        lraw2 = {}
+        lraw1 = {}
+        hw = {}
+
+        def load_l(g):
+            t2 = inp.tile([P, GB, 32], BF16, name="lraw2_%d" % g)
+            nc.sync.dma_start(out=t2[:, :, 0:31], in_=lv2[:, GB * g:GB * (g + 1), :])
+            lraw2[g] = t2
+            t1 = inp.tile([P, GB, 16], BF16, name="lraw1_%d" % g)
+            nc.sync.dma_start(out=t1[:, :, 0:15], in_=lv1[:, GB * g:GB * (g + 1), :])
+            lraw1[g] = t1
+
+        def load_h(g, cuts):
+            for h in range(2):
+                hw[(h, g)] = inp.tile([P, 2 * GB, 16], BF16, name="hw%d_%d" % (h, g))
+            for lo, hi in cuts:
+                for h in range(2):
+                    nc.sync.dma_start(out=hw[(h, g)][:, lo:hi, :], in_=hv[h][:, 2 * GB * g + lo:2 * GB * g + hi, :])
+
+        flat = out.rearrange("n i j -> (n i j)")
+
+        def scratch(g):
+            return flat[LS_BASE + g * LS_WORDS:LS_BASE + (g + 1) * LS_WORDS]
+
+        def l_prep(g):
+            lp = lpp.tile([P, 48, GB], BF16, name="lp")
+            nc.vector.memset(lp[:, 31, :], 1.0)
+            nc.vector.memset(lp[:, 47, :], 1.0)
+            nc.vector.tensor_copy(out=lp[:, 0:31, :], in_=lraw2[g][:, :, 0:31].rearrange("p n b -> p b n"))
+            nc.vector.tensor_copy(out=lp[:, 32:47, :], in_=lraw1[g][:, :, 0:15].rearrange("p n b -> p b n"))
+            lt = ps_l.tile([P, 6, P], BF16, name="lt")
+            for o in range(6):
+                nc.tensor.transpose(lt[:, o, :], lp[:, 8 * o:8 * o + 8, :].rearrange("p b n -> p (b n)"), ident_b[:])
+            lc = lpp.tile([P, 6, P, 2], BF16, name="lc")
+            nc.scalar.copy(out=lc[:], in_=lt[:].unsqueeze(3).to_broadcast([P, 6, P, 2]))
+            nc.sync.dma_start(
+                out=scratch(g).rearrange("(o m w) -> m o w", o=6, m=P, w=P),
+                in_=lc[:].rearrange("p o j e -> p o (j e)").bitcast(F32))
+
+        lreps = {}
+
+        def l_load(c):
+            g, c4 = c // 4, c % 4
+            src = scratch(g).rearrange("(s x n w) -> x s (n w)", s=3, x=16, n=GB, w=P)
+            lrep = lrp.tile([P, 3, CB * P], F32, name="lrep")
+            for r in (0, 4, 1, 5, 2, 6, 3, 7):
+                nc.sync.dma_start(out=lrep[r:P:8, :, :], in_=src[:, :, CB * P * c4:CB * P * (c4 + 1)])
+            lreps[c] = lrep
+
+        wv = W.rearrange("a b (u c e) d -> c a (b u) (e d)", u=2, c=8, e=2)
+        wraw = const.tile([P, 64, 64], BF16, name="wraw")
+        win = const.tile([P, 4096], BF16, name="win", align_bytes=64)
+        wq = const.tile([P, 1024], U32, name="wq", align_bytes=64)
+        ws = const.tile([P, 1024], U8, name="ws", align_bytes=64)
+        wr = wraw[:].rearrange("p x y -> p (x y)").rearrange(
+            "p (g b t u q e) -> p g u e b q t", g=2, b=16, t=4, u=2, q=8, e=2)
+        wo = win[:].rearrange("p (g u e b q t) -> p g u e b q t", g=2, u=2, e=2, b=16, q=8, t=4)
+
+        def w_regroup(g, vector):
+            for u in range(2):
+                for e in range(2):
+                    if vector:
+                        nc.vector.tensor_copy(out=wo[:, g, u, e], in_=wr[:, g, u, e])
+                    else:
+                        nc.scalar.copy(out=wo[:, g, u, e], in_=wr[:, g, u, e])
+
+        ys = {}
+        hbs = {}
+        st = {}
+
+        def y_copy(c, h):
+            g, c4 = c // 4, c % 4
+            y = yp.tile([P, 2 * CB, 16, 8], I32, name="y")
+            src = hw[(h, g)][:, 2 * CB * c4:2 * CB * (c4 + 1), :].bitcast(I32)
+            nc.vector.tensor_copy(out=y[:], in_=src.unsqueeze(2).to_broadcast([P, 2 * CB, 16, 8]))
+            ys[(c, h)] = y
+
+        def h_bank(k):
+            c, h, pr = k // 4, (k % 4) // 2, k % 2
+            y = ys[(c, h)]
+            hb = ps_h.tile([P, 4, P], F32, name="hb")
+            for i in range(4):
+                nc.tensor.transpose(hb[:, i, :], y[:, 4 * pr + i].rearrange("p b q -> p (b q)").bitcast(F32), ident_f[:])
+            hbs[k] = hb
+
+        def mult(dst, hb, lwords):
+            nc.vector.tensor_tensor(
+                out=dst.rearrange("p (c u e) -> p c u e", u=2, e=2),
+                in0=hb[:].rearrange("p k x -> p (k x)").bitcast(BF16).rearrange("p (c u e) -> p c u e", u=2, e=2),
+                in1=lwords.bitcast(BF16).rearrange("p (c e) -> p c e", e=2).unsqueeze(2).to_broadcast([P, 256, 2, 2]),
+                op=MULT)
+
+        def product(k):
+            c, h, pr = k // 4, (k % 4) // 2, k % 2
+            lrep = lreps[c]
+            if k % 4 == 0:
+                st[c] = {
+                    "p_in": work.tile([P, 2048], BF16, name="p_in", align_bytes=64),
+                    "r_in": work.tile([P, 2, 2048], BF16, name="r_in", align_bytes=64),
+                }
+            if h == 0:
+                mult(st[c]["p_in"][:, 1024 * pr:1024 * (pr + 1)], hbs[k], lrep[:, 2, 256 * pr:256 * (pr + 1)])
+            else:
+                for g in range(2):
+                    mult(st[c]["r_in"][:, g, 1024 * pr:1024 * (pr + 1)], hbs[k], lrep[:, g, 256 * pr:256 * (pr + 1)])
+
+        def quant(c, src, words, codes, scales):
+            cd = work.tile([P, words], U32, name=codes, align_bytes=64)
+            sc = work.tile([P, words], U8, name=scales, align_bytes=64)
+            nc.vector.quantize_mx(out=cd[:].bitcast(FP8X4), scales=sc[:], in_=src)
+            st[c][codes] = cd
+            st[c][scales] = sc
+
+        def mm1(c, units):
+            s = st[c]
+            if "q_in" not in s:
+                s["q_in"] = work.tile([P, 2 * CB, 512], BF16, name="q_in", align_bytes=64)
+            for un in units:
+                n, g = un // 2, un % 2
+                qb = ps_q.tile([P, 4, P], F32, name="qb")
+                for t in range(4):
+                    col = (4 * g + t) * P
+                    nc.tensor.matmul_mx(
+                        out=qb[:, t, :],
+                        lhsT=wq[:, col:col + P].bitcast(FP8X4), lhsT_scale=ws[:, col:col + P],
+                        rhs=s["pq"][:, P * n:P * (n + 1)].bitcast(FP8X4), rhs_scale=s["ps"][:, P * n:P * (n + 1)],
+                        start=True, stop=True)
+                nc.scalar.copy(out=s["q_in"][:, un, :].rearrange("p (i t) -> p i t", t=4),
+                               in_=qb[:].rearrange("p t i -> p i t"))
+
+        def mm2(c):
+            s = st[c]
+            ob = ps_o.tile([P, CB, P], F32, name="ob")
+            for n in range(CB):
+                for g in range(2):
+                    a = (2 * n + g) * P
+                    b = (CB * g + n) * P
+                    nc.tensor.matmul_mx(
+                        out=ob[:, n, :],
+                        lhsT=s["qq"][:, a:a + P].bitcast(FP8X4), lhsT_scale=s["qs"][:, a:a + P],
+                        rhs=s["rq"][:, b:b + P].bitcast(FP8X4), rhs_scale=s["rs"][:, b:b + P],
+                        start=(g == 0), stop=(g == 1))
+            osb = outp.tile([P, CB, P], F32, name="osb")
+            nc.scalar.copy(out=osb[:], in_=ob[:])
+            nc.scalar.dma_start(out=out[CB * c:CB * (c + 1)].rearrange("n i j -> i n j"), in_=osb[:])
+
+        def ok(c):
+            return 0 <= c < NCH
+
+        load_l(0)
+        load_h(0, [(0, 8), (8, 32)])
+        for c8 in range(8):
+            nc.scalar.dma_start(out=wraw[c8:P:8, :, :], in_=wv[c8])
+        l_prep(0)
+        l_load(0)
+        l_load(1)
+
+        for s in range(NU + 2 + 12):
+            if s % 4 == 2 and ok((s + 6) // 4) and (s + 6) // 4 >= 2:
+                l_load((s + 6) // 4)
+            if s % 16 == 2 and s // 16 + 1 < NG:
+                load_l(s // 16 + 1)
+                load_h(s // 16 + 1, [(0, 32)])
+            if s % 16 == 6 and s // 16 + 1 < NG:
+                l_prep(s // 16 + 1)
+            if s < NU and s % 2 == 0:
+                y_copy(s // 4, (s % 4) // 2)
+            if s == 2:
+                w_regroup(0, True)
+                w_regroup(1, False)
+                nc.vector.quantize_mx(out=wq[:].bitcast(FP8X4), scales=ws[:], in_=win[:])
+            k = s - 2
+            c, j = k // 4, k % 4
+            if k >= 0:
+                if j == 0:
+                    if ok(c - 1):
+                        mm1(c - 1, (2, 3))
+                    if ok(c - 2):
+                        mm2(c - 2)
+                elif j == 1:
+                    if ok(c - 1):
+                        mm1(c - 1, (4, 5))
+                elif j == 2:
+                    if ok(c - 1):
+                        mm1(c - 1, (6, 7))
+            if s < NU:
+                h_bank(s)
+            if k >= 0:
+                if ok(c):
+                    product(k)
+                if j == 0 and ok(c - 1):
+                    quant(c - 1, st[c - 1]["r_in"][:].rearrange("p g x -> p (g x)"), 1024, "rq", "rs")
+                if j == 2 and ok(c):
+                    quant(c, st[c]["p_in"][:], 512, "pq", "ps")
+                if j == 3:
+                    if ok(c - 1):
+                        quant(c - 1, st[c - 1]["q_in"][:].rearrange("p k x -> p (k x)"), 1024, "qq", "qs")
+                    if ok(c):
+                        mm1(c, (0, 1))

@@ -10,6 +10,7 @@ U32 = mybir.dt.uint32
 I32 = mybir.dt.int32
 FP8X4 = mybir.dt.float8_e4m3fn_x4
 MULT = mybir.AluOpType.mult
+ADD = mybir.AluOpType.add
 
 P = 128
 NB = 64
@@ -17,11 +18,11 @@ CB = 4
 NCH = NB // CB
 GB = 16
 NG = NB // GB
-NU = 4 * NCH
 FLOPS = 2 * 8192 * 512 * 1024 + 2 * 64 * 128 * 128 * 1024
 
 LS_WORDS = 48 * GB * 128
 LS_BASE = NB * P * P - NG * LS_WORDS
+N_DIRECT = 2
 
 
 def tile_qriaffine_t_kernel(tc, layer1, layer2, layer3, h1, h2, h3, W, out):
@@ -30,20 +31,20 @@ def tile_qriaffine_t_kernel(tc, layer1, layer2, layer3, h1, h2, h3, W, out):
         const = ctx.enter_context(tc.tile_pool(name="const", bufs=1))
         inp = ctx.enter_context(tc.tile_pool(name="inp", bufs=1))
         lpp = ctx.enter_context(tc.tile_pool(name="lpp", bufs=2))
+        zp = ctx.enter_context(tc.tile_pool(name="zp", bufs=6))
         yp = ctx.enter_context(tc.tile_pool(name="yp", bufs=2))
         lrp = ctx.enter_context(tc.tile_pool(name="lrp", bufs=3))
-        work = ctx.enter_context(tc.tile_pool(name="work", bufs=2))
+        work = ctx.enter_context(tc.tile_pool(name="work", bufs=3))
         outp = ctx.enter_context(tc.tile_pool(name="outp", bufs=3))
         ps_h = ctx.enter_context(tc.psum_pool(name="ps_h", bufs=3))
-        ps_q = ctx.enter_context(tc.psum_pool(name="ps_q", bufs=3))
+        ps_q = ctx.enter_context(tc.psum_pool(name="ps_q", bufs=4))
         ps_o = ctx.enter_context(tc.psum_pool(name="ps_o", bufs=1))
-        ps_l = ctx.enter_context(tc.psum_pool(name="ps_l", bufs=1))
         ctx.enter_context(tc.manual_schedule())
 
-        ident_b = const.tile([P, P], BF16, name="ident_b")
-        make_identity(nc, ident_b[:])
         ident_f = const.tile([P, P], F32, name="ident_f")
         make_identity(nc, ident_f[:])
+        ident_b = const.tile([P, P], BF16, name="ident_b")
+        make_identity(nc, ident_b[:])
 
         lv2 = layer2.rearrange("n j b -> j n b")
         lv1 = layer1.rearrange("n j b -> j n b")
@@ -55,6 +56,9 @@ def tile_qriaffine_t_kernel(tc, layer1, layer2, layer3, h1, h2, h3, W, out):
         lraw1 = {}
         hw = {}
 
+        def ok(c):
+            return 0 <= c < NCH
+
         def load_l(g):
             t2 = inp.tile([P, GB, 32], BF16, name="lraw2_%d" % g)
             nc.sync.dma_start(out=t2[:, :, 0:31], in_=lv2[:, GB * g:GB * (g + 1), :])
@@ -63,12 +67,11 @@ def tile_qriaffine_t_kernel(tc, layer1, layer2, layer3, h1, h2, h3, W, out):
             nc.sync.dma_start(out=t1[:, :, 0:15], in_=lv1[:, GB * g:GB * (g + 1), :])
             lraw1[g] = t1
 
-        def load_h(g, cuts):
+        def load_h(g, lo, hi):
             for h in range(2):
-                hw[(h, g)] = inp.tile([P, 2 * GB, 16], BF16, name="hw%d_%d" % (h, g))
-            for lo, hi in cuts:
-                for h in range(2):
-                    nc.sync.dma_start(out=hw[(h, g)][:, lo:hi, :], in_=hv[h][:, 2 * GB * g + lo:2 * GB * g + hi, :])
+                if (h, g) not in hw:
+                    hw[(h, g)] = inp.tile([P, 2 * GB, 16], BF16, name="hw%d_%d" % (h, g))
+                nc.sync.dma_start(out=hw[(h, g)][:, lo:hi, :], in_=hv[h][:, 2 * GB * g + lo:2 * GB * g + hi, :])
 
         flat = out.rearrange("n i j -> (n i j)")
 
@@ -81,7 +84,7 @@ def tile_qriaffine_t_kernel(tc, layer1, layer2, layer3, h1, h2, h3, W, out):
             nc.vector.memset(lp[:, 47, :], 1.0)
             nc.vector.tensor_copy(out=lp[:, 0:31, :], in_=lraw2[g][:, :, 0:31].rearrange("p n b -> p b n"))
             nc.vector.tensor_copy(out=lp[:, 32:47, :], in_=lraw1[g][:, :, 0:15].rearrange("p n b -> p b n"))
-            lt = ps_l.tile([P, 6, P], BF16, name="lt")
+            lt = ps_q.tile([P, 6, P], BF16, name="lt", tag="qb")
             for o in range(6):
                 nc.tensor.transpose(lt[:, o, :], lp[:, 8 * o:8 * o + 8, :].rearrange("p b n -> p (b n)"), ident_b[:])
             lc = lpp.tile([P, 6, P, 2], BF16, name="lc")
@@ -93,12 +96,30 @@ def tile_qriaffine_t_kernel(tc, layer1, layer2, layer3, h1, h2, h3, W, out):
         lreps = {}
 
         def l_load(c):
+            if not ok(c):
+                return
             g, c4 = c // 4, c % 4
             src = scratch(g).rearrange("(s x n w) -> x s (n w)", s=3, x=16, n=GB, w=P)
             lrep = lrp.tile([P, 3, CB * P], F32, name="lrep")
             for r in (0, 4, 1, 5, 2, 6, 3, 7):
                 nc.sync.dma_start(out=lrep[r:P:8, :, :], in_=src[:, :, CB * P * c4:CB * P * (c4 + 1)])
             lreps[c] = lrep
+
+        def l_direct(c, s):
+            if c not in lreps:
+                lreps[c] = lrp.tile([P, 3, CB * P], F32, name="lrep")
+            z = zp.tile([P, CB, 16, 16], BF16, name="z")
+            n0 = CB * c
+            if s == 0:
+                nc.vector.tensor_copy(out=z[:], in_=lraw2[0][:, n0:n0 + CB, 0:16].unsqueeze(3).to_broadcast([P, CB, 16, 16]))
+            else:
+                src = lraw2[0][:, n0:n0 + CB, 16:31] if s == 1 else lraw1[0][:, n0:n0 + CB, 0:15]
+                nc.vector.memset(z[:, :, 15, :], 1.0)
+                nc.vector.tensor_copy(out=z[:, :, 0:15, :], in_=src.unsqueeze(3).to_broadcast([P, CB, 15, 16]))
+            zb = ps_q.tile([P, CB, P], F32, name="zb", tag="qb")
+            for n in range(CB):
+                nc.tensor.transpose(zb[:, n, :], z[:, n].rearrange("p x e -> p (x e)").bitcast(F32), ident_f[:])
+            nc.scalar.copy(out=lreps[c][:, s, :], in_=zb[:].rearrange("p n j -> p (n j)"))
 
         wv = W.rearrange("a b (u c e) d -> c a (b u) (e d)", u=2, c=8, e=2)
         wraw = const.tile([P, 64, 64], BF16, name="wraw")
@@ -109,27 +130,26 @@ def tile_qriaffine_t_kernel(tc, layer1, layer2, layer3, h1, h2, h3, W, out):
             "p (g b t u q e) -> p g u e b q t", g=2, b=16, t=4, u=2, q=8, e=2)
         wo = win[:].rearrange("p (g u e b q t) -> p g u e b q t", g=2, u=2, e=2, b=16, q=8, t=4)
 
-        def w_regroup(g, vector):
-            for u in range(2):
-                for e in range(2):
-                    if vector:
-                        nc.vector.tensor_copy(out=wo[:, g, u, e], in_=wr[:, g, u, e])
-                    else:
-                        nc.scalar.copy(out=wo[:, g, u, e], in_=wr[:, g, u, e])
-
         ys = {}
         hbs = {}
         st = {}
 
         def y_copy(c, h):
+            if not ok(c):
+                return
             g, c4 = c // 4, c % 4
-            y = yp.tile([P, 2 * CB, 16, 8], I32, name="y")
-            src = hw[(h, g)][:, 2 * CB * c4:2 * CB * (c4 + 1), :].bitcast(I32)
-            nc.vector.tensor_copy(out=y[:], in_=src.unsqueeze(2).to_broadcast([P, 2 * CB, 16, 8]))
+            y = yp.tile([P, 2 * CB, 16, 8], I32, name="y%d" % h)
+            src = hw[(h, g)][:, 2 * CB * c4:2 * CB * (c4 + 1), :]
+            if h == 0:
+                nc.scalar.copy(out=y[:].bitcast(F32), in_=src.bitcast(F32).unsqueeze(2).to_broadcast([P, 2 * CB, 16, 8]))
+            else:
+                nc.vector.tensor_copy(out=y[:], in_=src.bitcast(I32).unsqueeze(2).to_broadcast([P, 2 * CB, 16, 8]))
             ys[(c, h)] = y
 
         def h_bank(k):
             c, h, pr = k // 4, (k % 4) // 2, k % 2
+            if not ok(c):
+                return
             y = ys[(c, h)]
             hb = ps_h.tile([P, 4, P], F32, name="hb")
             for i in range(4):
@@ -145,6 +165,8 @@ def tile_qriaffine_t_kernel(tc, layer1, layer2, layer3, h1, h2, h3, W, out):
 
         def product(k):
             c, h, pr = k // 4, (k % 4) // 2, k % 2
+            if not ok(c):
+                return
             lrep = lreps[c]
             if k % 4 == 0:
                 st[c] = {
@@ -157,7 +179,16 @@ def tile_qriaffine_t_kernel(tc, layer1, layer2, layer3, h1, h2, h3, W, out):
                 for g in range(2):
                     mult(st[c]["r_in"][:, g, 1024 * pr:1024 * (pr + 1)], hbs[k], lrep[:, g, 256 * pr:256 * (pr + 1)])
 
-        def quant(c, src, words, codes, scales):
+        def quant(c, key, words, codes, scales):
+            if not ok(c):
+                return
+            src = st[c][key]
+            if key == "r_in":
+                src = src[:].rearrange("p g x -> p (g x)")
+            elif key == "q_in":
+                src = src[:].rearrange("p k x -> p (k x)")
+            else:
+                src = src[:]
             cd = work.tile([P, words], U32, name=codes, align_bytes=64)
             sc = work.tile([P, words], U8, name=scales, align_bytes=64)
             nc.vector.quantize_mx(out=cd[:].bitcast(FP8X4), scales=sc[:], in_=src)
@@ -165,6 +196,8 @@ def tile_qriaffine_t_kernel(tc, layer1, layer2, layer3, h1, h2, h3, W, out):
             st[c][scales] = sc
 
         def mm1(c, units):
+            if not ok(c):
+                return
             s = st[c]
             if "q_in" not in s:
                 s["q_in"] = work.tile([P, 2 * CB, 512], BF16, name="q_in", align_bytes=64)
@@ -182,6 +215,8 @@ def tile_qriaffine_t_kernel(tc, layer1, layer2, layer3, h1, h2, h3, W, out):
                                in_=qb[:].rearrange("p t i -> p i t"))
 
         def mm2(c):
+            if not ok(c):
+                return
             s = st[c]
             ob = ps_o.tile([P, CB, P], F32, name="ob")
             for n in range(CB):
@@ -197,56 +232,61 @@ def tile_qriaffine_t_kernel(tc, layer1, layer2, layer3, h1, h2, h3, W, out):
             nc.scalar.copy(out=osb[:], in_=ob[:])
             nc.scalar.dma_start(out=out[CB * c:CB * (c + 1)].rearrange("n i j -> i n j"), in_=osb[:])
 
-        def ok(c):
-            return 0 <= c < NCH
-
         load_l(0)
-        load_h(0, [(0, 8), (8, 32)])
+        load_h(0, 0, 8)
         for c8 in range(8):
-            nc.scalar.dma_start(out=wraw[c8:P:8, :, :], in_=wv[c8])
+            nc.sync.dma_start(out=wraw[c8:P:8, :, :], in_=wv[c8])
+        load_h(0, 8, 32)
+        load_l(1)
+        y_copy(0, 0)
+        l_direct(0, 2)
+        h_bank(0)
+        h_bank(1)
+        l_direct(0, 0)
+        l_direct(0, 1)
+        y_copy(0, 1)
+        h_bank(2)
         l_prep(0)
-        l_load(0)
-        l_load(1)
+        for s in (2, 0, 1):
+            l_direct(1, s)
+        l_load(2)
+        load_h(1, 0, 32)
+        y_copy(1, 0)
+        for g in range(2):
+            for u in range(2):
+                for e in range(2):
+                    nc.gpsimd.tensor_scalar(out=wo[:, g, u, e], in0=wr[:, g, u, e], scalar1=1.0, scalar2=0.0, op0=MULT, op1=ADD)
 
-        for s in range(NU + 2 + 12):
-            if s % 4 == 2 and ok((s + 6) // 4) and (s + 6) // 4 >= 2:
-                l_load((s + 6) // 4)
-            if s % 16 == 2 and s // 16 + 1 < NG:
-                load_l(s // 16 + 1)
-                load_h(s // 16 + 1, [(0, 32)])
-            if s % 16 == 6 and s // 16 + 1 < NG:
-                l_prep(s // 16 + 1)
-            if s < NU and s % 2 == 0:
-                y_copy(s // 4, (s % 4) // 2)
-            if s == 2:
-                w_regroup(0, True)
-                w_regroup(1, False)
+        for c in range(NCH + 4):
+            if (c + 6) % 4 == 0 and 2 <= (c + 6) // 4 < NG:
+                load_l((c + 6) // 4)
+                load_h((c + 6) // 4, 0, 32)
+            if (c + 3) % 4 == 0 and (c + 3) // 4 < NG:
+                l_prep((c + 3) // 4)
+            if c == 1:
                 nc.vector.quantize_mx(out=wq[:].bitcast(FP8X4), scales=ws[:], in_=win[:])
-            k = s - 2
-            c, j = k // 4, k % 4
-            if k >= 0:
-                if j == 0:
-                    if ok(c - 1):
-                        mm1(c - 1, (2, 3))
-                    if ok(c - 2):
-                        mm2(c - 2)
-                elif j == 1:
-                    if ok(c - 1):
-                        mm1(c - 1, (4, 5))
-                elif j == 2:
-                    if ok(c - 1):
-                        mm1(c - 1, (6, 7))
-            if s < NU:
-                h_bank(s)
-            if k >= 0:
-                if ok(c):
-                    product(k)
-                if j == 0 and ok(c - 1):
-                    quant(c - 1, st[c - 1]["r_in"][:].rearrange("p g x -> p (g x)"), 1024, "rq", "rs")
-                if j == 2 and ok(c):
-                    quant(c, st[c]["p_in"][:], 512, "pq", "ps")
-                if j == 3:
-                    if ok(c - 1):
-                        quant(c - 1, st[c - 1]["q_in"][:].rearrange("p k x -> p (k x)"), 1024, "qq", "qs")
-                    if ok(c):
-                        mm1(c, (0, 1))
+            product(4 * c)
+            if c == 1:
+                mm1(0, (0, 1, 2, 3))
+            mm1(c - 1, (4, 5))
+            h_bank(4 * c + 3)
+            product(4 * c + 1)
+            mm1(c - 1, (6,))
+            h_bank(4 * c + 4)
+            mm1(c - 1, (7,))
+            y_copy(c + 1, 1)
+            y_copy(c + 2, 0)
+            quant(c - 1, "r_in", 1024, "rq", "rs")
+            product(4 * c + 2)
+            h_bank(4 * c + 5)
+            quant(c, "p_in", 512, "pq", "ps")
+            if c > 0:
+                mm1(c, (0, 1, 2))
+            mm2(c - 3)
+            product(4 * c + 3)
+            if ok(c):
+                l_load(c + 3)
+            h_bank(4 * c + 6)
+            if c > 0:
+                mm1(c, (3,))
+            quant(c - 2, "q_in", 1024, "qq", "qs")

@@ -18,11 +18,14 @@ CB = 4
 NCH = NB // CB
 GB = 16
 NG = NB // GB
+UB = 8
+NUN = NB // UB
 FLOPS = 2 * 8192 * 512 * 1024 + 2 * 64 * 128 * 128 * 1024
 
-LS_WORDS = 48 * GB * 128
+L2_WORDS = 16 * GB * 2 * 128
+L1_WORDS = 16 * GB * 128
+LS_WORDS = L2_WORDS + L1_WORDS
 LS_BASE = NB * P * P - NG * LS_WORDS
-N_DIRECT = 2
 
 
 def tile_qriaffine_t_kernel(tc, layer1, layer2, layer3, h1, h2, h3, W, out):
@@ -36,9 +39,8 @@ def tile_qriaffine_t_kernel(tc, layer1, layer2, layer3, h1, h2, h3, W, out):
         lrp = ctx.enter_context(tc.tile_pool(name="lrp", bufs=3))
         work = ctx.enter_context(tc.tile_pool(name="work", bufs=3))
         outp = ctx.enter_context(tc.tile_pool(name="outp", bufs=3))
-        ps_h = ctx.enter_context(tc.psum_pool(name="ps_h", bufs=3))
+        ps_h = ctx.enter_context(tc.psum_pool(name="ps_h", bufs=4))
         ps_q = ctx.enter_context(tc.psum_pool(name="ps_q", bufs=4))
-        ps_o = ctx.enter_context(tc.psum_pool(name="ps_o", bufs=1))
         ctx.enter_context(tc.manual_schedule())
 
         ident_f = const.tile([P, P], F32, name="ident_f")
@@ -75,39 +77,54 @@ def tile_qriaffine_t_kernel(tc, layer1, layer2, layer3, h1, h2, h3, W, out):
 
         flat = out.rearrange("n i j -> (n i j)")
 
-        def scratch(g):
-            return flat[LS_BASE + g * LS_WORDS:LS_BASE + (g + 1) * LS_WORDS]
+        def scratch2(g):
+            lo = LS_BASE + g * LS_WORDS
+            return flat[lo:lo + L2_WORDS]
+
+        def scratch1(g):
+            lo = LS_BASE + g * LS_WORDS + L2_WORDS
+            return flat[lo:lo + L1_WORDS]
 
         def l_prep(g):
             lp = lpp.tile([P, 48, GB], BF16, name="lp")
-            nc.vector.memset(lp[:, 31, :], 1.0)
-            nc.vector.memset(lp[:, 47, :], 1.0)
-            nc.vector.tensor_copy(out=lp[:, 0:31, :], in_=lraw2[g][:, :, 0:31].rearrange("p n b -> p b n"))
-            nc.vector.tensor_copy(out=lp[:, 32:47, :], in_=lraw1[g][:, :, 0:15].rearrange("p n b -> p b n"))
+            nc.gpsimd.memset(lp[:, 31, :], 1.0)
+            nc.gpsimd.memset(lp[:, 47, :], 1.0)
+            nc.gpsimd.tensor_scalar(out=lp[:, 0:31, :], in0=lraw2[g][:, :, 0:31].rearrange("p n b -> p b n"),
+                                    scalar1=1.0, scalar2=0.0, op0=MULT, op1=ADD)
+            nc.gpsimd.tensor_scalar(out=lp[:, 32:47, :], in0=lraw1[g][:, :, 0:15].rearrange("p n b -> p b n"),
+                                    scalar1=1.0, scalar2=0.0, op0=MULT, op1=ADD)
             lt = ps_q.tile([P, 6, P], BF16, name="lt", tag="qb")
             for o in range(6):
                 nc.tensor.transpose(lt[:, o, :], lp[:, 8 * o:8 * o + 8, :].rearrange("p b n -> p (b n)"), ident_b[:])
             lc = lpp.tile([P, 6, P, 2], BF16, name="lc")
             nc.scalar.copy(out=lc[:], in_=lt[:].unsqueeze(3).to_broadcast([P, 6, P, 2]))
-            nc.sync.dma_start(
-                out=scratch(g).rearrange("(o m w) -> m o w", o=6, m=P, w=P),
-                in_=lc[:].rearrange("p o j e -> p o (j e)").bitcast(F32))
+            lcw = lc[:].rearrange("p o j e -> p o (j e)").bitcast(F32)
+            d2 = scratch2(g).rearrange("(xh b n g w) -> g (b n) xh w", xh=2, b=8, n=GB, g=2, w=P)
+            for gg in range(2):
+                nc.sync.dma_start(out=d2[gg], in_=lcw[:, 2 * gg:2 * gg + 2, :])
+            nc.sync.dma_start(out=scratch1(g).rearrange("(xh b n w) -> (b n) xh w", xh=2, b=8, n=GB, w=P), in_=lcw[:, 4:6, :])
 
-        lreps = {}
+        lrep2 = {}
+        lrep1 = {}
 
-        def l_load(c):
-            if not ok(c):
+        def l_tiles(un):
+            if un not in lrep2:
+                lrep2[un] = lrp.tile([P, UB * 2 * P], F32, name="lrep2")
+                lrep1[un] = lrp.tile([P, UB * P], F32, name="lrep1")
+
+        def l_load(un):
+            if not 0 <= un < NUN:
                 return
-            g, c4 = c // 4, c % 4
-            src = scratch(g).rearrange("(s x n w) -> x s (n w)", s=3, x=16, n=GB, w=P)
-            lrep = lrp.tile([P, 3, CB * P], F32, name="lrep")
+            g, half = un // 2, un % 2
+            l_tiles(un)
+            s2 = scratch2(g).rearrange("(x m) -> x m", x=16)[:, 2048 * half:2048 * (half + 1)]
+            s1 = scratch1(g).rearrange("(x m) -> x m", x=16)[:, 1024 * half:1024 * (half + 1)]
             for r in (0, 4, 1, 5, 2, 6, 3, 7):
-                nc.sync.dma_start(out=lrep[r:P:8, :, :], in_=src[:, :, CB * P * c4:CB * P * (c4 + 1)])
-            lreps[c] = lrep
+                nc.sync.dma_start(out=lrep1[un][r:P:8, :], in_=s1)
+                nc.sync.dma_start(out=lrep2[un][r:P:8, :], in_=s2)
 
         def l_direct(c, s):
-            if c not in lreps:
-                lreps[c] = lrp.tile([P, 3, CB * P], F32, name="lrep")
+            l_tiles(0)
             z = zp.tile([P, CB, 16, 16], BF16, name="z")
             n0 = CB * c
             if s == 0:
@@ -119,7 +136,11 @@ def tile_qriaffine_t_kernel(tc, layer1, layer2, layer3, h1, h2, h3, W, out):
             zb = ps_q.tile([P, CB, P], F32, name="zb", tag="qb")
             for n in range(CB):
                 nc.tensor.transpose(zb[:, n, :], z[:, n].rearrange("p x e -> p (x e)").bitcast(F32), ident_f[:])
-            nc.scalar.copy(out=lreps[c][:, s, :], in_=zb[:].rearrange("p n j -> p (n j)"))
+            if s == 2:
+                nc.scalar.copy(out=lrep1[0][:, CB * P * c:CB * P * (c + 1)].rearrange("p (n j) -> p n j", n=CB), in_=zb[:])
+            else:
+                dst = lrep2[0][:].rearrange("p (n g j) -> p n g j", n=UB, g=2, j=P)
+                nc.scalar.copy(out=dst[:, n0:n0 + CB, s, :], in_=zb[:])
 
         wv = W.rearrange("a b (u c e) d -> c a (b u) (e d)", u=2, c=8, e=2)
         wraw = const.tile([P, 64, 64], BF16, name="wraw")
@@ -146,46 +167,51 @@ def tile_qriaffine_t_kernel(tc, layer1, layer2, layer3, h1, h2, h3, W, out):
                 nc.vector.tensor_copy(out=y[:], in_=src.bitcast(I32).unsqueeze(2).to_broadcast([P, 2 * CB, 16, 8]))
             ys[(c, h)] = y
 
-        def h_bank(k):
-            c, h, pr = k // 4, (k % 4) // 2, k % 2
+        def h_banks(c, h):
             if not ok(c):
                 return
             y = ys[(c, h)]
-            hb = ps_h.tile([P, 4, P], F32, name="hb")
-            for i in range(4):
-                nc.tensor.transpose(hb[:, i, :], y[:, 4 * pr + i].rearrange("p b q -> p (b q)").bitcast(F32), ident_f[:])
-            hbs[k] = hb
+            for pr in range(2):
+                hb = ps_h.tile([P, 4, P], F32, name="hb")
+                for i in range(4):
+                    nc.tensor.transpose(hb[:, i, :], y[:, 4 * pr + i].rearrange("p b q -> p (b q)").bitcast(F32), ident_f[:])
+                hbs[(c, h, pr)] = hb
 
-        def mult(dst, hb, lwords):
-            nc.vector.tensor_tensor(
-                out=dst.rearrange("p (c u e) -> p c u e", u=2, e=2),
-                in0=hb[:].rearrange("p k x -> p (k x)").bitcast(BF16).rearrange("p (c u e) -> p c u e", u=2, e=2),
-                in1=lwords.bitcast(BF16).rearrange("p (c e) -> p c e", e=2).unsqueeze(2).to_broadcast([P, 256, 2, 2]),
-                op=MULT)
-
-        def product(k):
-            c, h, pr = k // 4, (k % 4) // 2, k % 2
+        def prod_p(c, pr):
             if not ok(c):
                 return
-            lrep = lreps[c]
-            if k % 4 == 0:
-                st[c] = {
-                    "p_in": work.tile([P, 2048], BF16, name="p_in", align_bytes=64),
-                    "r_in": work.tile([P, 2, 2048], BF16, name="r_in", align_bytes=64),
-                }
-            if h == 0:
-                mult(st[c]["p_in"][:, 1024 * pr:1024 * (pr + 1)], hbs[k], lrep[:, 2, 256 * pr:256 * (pr + 1)])
-            else:
-                for g in range(2):
-                    mult(st[c]["r_in"][:, g, 1024 * pr:1024 * (pr + 1)], hbs[k], lrep[:, g, 256 * pr:256 * (pr + 1)])
+            if c not in st:
+                st[c] = {}
+            if pr == 0:
+                st[c]["p_in"] = work.tile([P, 2048], BF16, name="p_in", align_bytes=64)
+            nl = CB * (c % 2) + 2 * pr
+            nc.vector.tensor_tensor(
+                out=st[c]["p_in"][:, 1024 * pr:1024 * (pr + 1)].rearrange("p (c u e) -> p c u e", u=2, e=2),
+                in0=hbs[(c, 0, pr)][:].rearrange("p k x -> p (k x)").bitcast(BF16).rearrange("p (c u e) -> p c u e", u=2, e=2),
+                in1=lrep1[c // 2][:, P * nl:P * (nl + 2)].bitcast(BF16).rearrange("p (c e) -> p c e", e=2)
+                .unsqueeze(2).to_broadcast([P, 256, 2, 2]),
+                op=MULT)
+
+        def prod_r(c, pr):
+            if not ok(c):
+                return
+            if pr == 0:
+                st[c]["r_in"] = work.tile([P, 4096], BF16, name="r_in", align_bytes=64)
+            nl = CB * (c % 2) + 2 * pr
+            shape = [P, 2, 2, P, 2, 2]
+            nc.vector.tensor_tensor(
+                out=st[c]["r_in"][:, 2048 * pr:2048 * (pr + 1)].rearrange("p (n g j u e) -> p n g j u e", n=2, g=2, j=P, u=2, e=2),
+                in0=hbs[(c, 1, pr)][:].rearrange("p k x -> p (k x)").bitcast(BF16)
+                .rearrange("p (n j u e) -> p n j u e", n=2, j=P, u=2, e=2).unsqueeze(2).to_broadcast(shape),
+                in1=lrep2[c // 2][:, 2 * P * nl:2 * P * (nl + 2)].bitcast(BF16)
+                .rearrange("p (n g j e) -> p n g j e", n=2, g=2, j=P, e=2).unsqueeze(4).to_broadcast(shape),
+                op=MULT)
 
         def quant(c, key, words, codes, scales):
             if not ok(c):
                 return
             src = st[c][key]
-            if key == "r_in":
-                src = src[:].rearrange("p g x -> p (g x)")
-            elif key == "q_in":
+            if key == "q_in":
                 src = src[:].rearrange("p k x -> p (k x)")
             else:
                 src = src[:]
@@ -218,38 +244,37 @@ def tile_qriaffine_t_kernel(tc, layer1, layer2, layer3, h1, h2, h3, W, out):
             if not ok(c):
                 return
             s = st[c]
-            ob = ps_o.tile([P, CB, P], F32, name="ob")
+            ob = ps_q.tile([P, CB, P], F32, name="ob", tag="qb")
             for n in range(CB):
                 for g in range(2):
                     a = (2 * n + g) * P
-                    b = (CB * g + n) * P
                     nc.tensor.matmul_mx(
                         out=ob[:, n, :],
                         lhsT=s["qq"][:, a:a + P].bitcast(FP8X4), lhsT_scale=s["qs"][:, a:a + P],
-                        rhs=s["rq"][:, b:b + P].bitcast(FP8X4), rhs_scale=s["rs"][:, b:b + P],
+                        rhs=s["rq"][:, a:a + P].bitcast(FP8X4), rhs_scale=s["rs"][:, a:a + P],
                         start=(g == 0), stop=(g == 1))
             osb = outp.tile([P, CB, P], F32, name="osb")
             nc.scalar.copy(out=osb[:], in_=ob[:])
-            nc.scalar.dma_start(out=out[CB * c:CB * (c + 1)].rearrange("n i j -> i n j"), in_=osb[:])
+            nc.sync.dma_start(out=out[CB * c:CB * (c + 1)].rearrange("n i j -> i n j"), in_=osb[:])
 
         load_l(0)
         load_h(0, 0, 8)
+        load_h(0, 8, 16)
         for c8 in range(8):
             nc.sync.dma_start(out=wraw[c8:P:8, :, :], in_=wv[c8])
-        load_h(0, 8, 32)
+        load_h(0, 16, 32)
         load_l(1)
         y_copy(0, 0)
         l_direct(0, 2)
-        h_bank(0)
-        h_bank(1)
+        h_banks(0, 0)
         l_direct(0, 0)
         l_direct(0, 1)
         y_copy(0, 1)
-        h_bank(2)
+        h_banks(0, 1)
         l_prep(0)
         for s in (2, 0, 1):
             l_direct(1, s)
-        l_load(2)
+        l_load(1)
         load_h(1, 0, 32)
         y_copy(1, 0)
         for g in range(2):
@@ -265,28 +290,25 @@ def tile_qriaffine_t_kernel(tc, layer1, layer2, layer3, h1, h2, h3, W, out):
                 l_prep((c + 3) // 4)
             if c == 1:
                 nc.vector.quantize_mx(out=wq[:].bitcast(FP8X4), scales=ws[:], in_=win[:])
-            product(4 * c)
+            prod_p(c, 0)
             if c == 1:
                 mm1(0, (0, 1, 2, 3))
             mm1(c - 1, (4, 5))
-            h_bank(4 * c + 3)
-            product(4 * c + 1)
-            mm1(c - 1, (6,))
-            h_bank(4 * c + 4)
-            mm1(c - 1, (7,))
+            prod_p(c, 1)
+            h_banks(c + 1, 0)
+            mm1(c - 1, (6, 7))
             y_copy(c + 1, 1)
             y_copy(c + 2, 0)
             quant(c - 1, "r_in", 1024, "rq", "rs")
-            product(4 * c + 2)
-            h_bank(4 * c + 5)
+            prod_r(c, 0)
             quant(c, "p_in", 512, "pq", "ps")
             if c > 0:
                 mm1(c, (0, 1, 2))
             mm2(c - 3)
-            product(4 * c + 3)
-            if ok(c):
-                l_load(c + 3)
-            h_bank(4 * c + 6)
+            prod_r(c, 1)
+            if ok(c) and c % 2 == 1:
+                l_load((c + 1) // 2 + 1)
+            h_banks(c + 1, 1)
             if c > 0:
                 mm1(c, (3,))
             quant(c - 2, "q_in", 1024, "qq", "qs")

@@ -38,7 +38,7 @@ def tile_qriaffine_t_kernel(tc, layer1, layer2, layer3, h1, h2, h3, W, out):
         yp = ctx.enter_context(tc.tile_pool(name="yp", bufs=2))
         lrp = ctx.enter_context(tc.tile_pool(name="lrp", bufs=3))
         work = ctx.enter_context(tc.tile_pool(name="work", bufs=3))
-        outp = ctx.enter_context(tc.tile_pool(name="outp", bufs=3))
+        outp = ctx.enter_context(tc.tile_pool(name="outp", bufs=5))
         ps_h = ctx.enter_context(tc.psum_pool(name="ps_h", bufs=4))
         ps_q = ctx.enter_context(tc.psum_pool(name="ps_q", bufs=4))
         ctx.enter_context(tc.manual_schedule())
@@ -61,13 +61,12 @@ def tile_qriaffine_t_kernel(tc, layer1, layer2, layer3, h1, h2, h3, W, out):
         def ok(c):
             return 0 <= c < NCH
 
-        def load_l(g):
-            t2 = inp.tile([P, GB, 32], BF16, name="lraw2_%d" % g)
-            nc.sync.dma_start(out=t2[:, :, 0:31], in_=lv2[:, GB * g:GB * (g + 1), :])
-            lraw2[g] = t2
-            t1 = inp.tile([P, GB, 16], BF16, name="lraw1_%d" % g)
-            nc.sync.dma_start(out=t1[:, :, 0:15], in_=lv1[:, GB * g:GB * (g + 1), :])
-            lraw1[g] = t1
+        def load_l(g, lo, hi):
+            if g not in lraw2:
+                lraw2[g] = inp.tile([P, GB, 32], BF16, name="lraw2_%d" % g)
+                lraw1[g] = inp.tile([P, GB, 16], BF16, name="lraw1_%d" % g)
+            nc.sync.dma_start(out=lraw1[g][:, lo:hi, 0:15], in_=lv1[:, GB * g + lo:GB * g + hi, :])
+            nc.sync.dma_start(out=lraw2[g][:, lo:hi, 0:31], in_=lv2[:, GB * g + lo:GB * g + hi, :])
 
         def load_h(g, lo, hi):
             for h in range(2):
@@ -124,9 +123,11 @@ def tile_qriaffine_t_kernel(tc, layer1, layer2, layer3, h1, h2, h3, W, out):
                 nc.sync.dma_start(out=lrep2[un][r:P:8, :], in_=s2)
 
         def l_direct(c, s):
-            l_tiles(0)
+            un = c // 2
+            l_tiles(un)
             z = zp.tile([P, CB, 16, 16], BF16, name="z")
             n0 = CB * c
+            m0 = CB * (c % 2)
             if s == 0:
                 nc.vector.tensor_copy(out=z[:], in_=lraw2[0][:, n0:n0 + CB, 0:16].unsqueeze(3).to_broadcast([P, CB, 16, 16]))
             else:
@@ -137,10 +138,10 @@ def tile_qriaffine_t_kernel(tc, layer1, layer2, layer3, h1, h2, h3, W, out):
             for n in range(CB):
                 nc.tensor.transpose(zb[:, n, :], z[:, n].rearrange("p x e -> p (x e)").bitcast(F32), ident_f[:])
             if s == 2:
-                nc.scalar.copy(out=lrep1[0][:, CB * P * c:CB * P * (c + 1)].rearrange("p (n j) -> p n j", n=CB), in_=zb[:])
+                nc.scalar.copy(out=lrep1[un][:, P * m0:P * (m0 + CB)].rearrange("p (n j) -> p n j", n=CB), in_=zb[:])
             else:
-                dst = lrep2[0][:].rearrange("p (n g j) -> p n g j", n=UB, g=2, j=P)
-                nc.scalar.copy(out=dst[:, n0:n0 + CB, s, :], in_=zb[:])
+                dst = lrep2[un][:].rearrange("p (n g j) -> p n g j", n=UB, g=2, j=P)
+                nc.scalar.copy(out=dst[:, m0:m0 + CB, s, :], in_=zb[:])
 
         wv = W.rearrange("a b (u c e) d -> c a (b u) (e d)", u=2, c=8, e=2)
         wraw = const.tile([P, 64, 64], BF16, name="wraw")
@@ -240,12 +241,21 @@ def tile_qriaffine_t_kernel(tc, layer1, layer2, layer3, h1, h2, h3, W, out):
                 nc.scalar.copy(out=s["q_in"][:, un, :].rearrange("p (i t) -> p i t", t=4),
                                in_=qb[:].rearrange("p t i -> p i t"))
 
-        def mm2(c):
+        def quant_q_half(c, hf):
+            s = st[c]
+            if hf == 0:
+                s["qq"] = work.tile([P, 1024], U32, name="qq", align_bytes=64)
+                s["qs"] = work.tile([P, 1024], U8, name="qs", align_bytes=64)
+            nc.vector.quantize_mx(
+                out=s["qq"][:, 512 * hf:512 * (hf + 1)].bitcast(FP8X4), scales=s["qs"][:, 512 * hf:512 * (hf + 1)],
+                in_=s["q_in"][:].rearrange("p k x -> p (k x)")[:, 2048 * hf:2048 * (hf + 1)])
+
+        def mm2(c, lo=0, hi=CB, vector=False):
             if not ok(c):
                 return
             s = st[c]
             ob = ps_q.tile([P, CB, P], F32, name="ob", tag="qb")
-            for n in range(CB):
+            for n in range(lo, hi):
                 for g in range(2):
                     a = (2 * n + g) * P
                     nc.tensor.matmul_mx(
@@ -254,16 +264,21 @@ def tile_qriaffine_t_kernel(tc, layer1, layer2, layer3, h1, h2, h3, W, out):
                         rhs=s["rq"][:, a:a + P].bitcast(FP8X4), rhs_scale=s["rs"][:, a:a + P],
                         start=(g == 0), stop=(g == 1))
             osb = outp.tile([P, CB, P], F32, name="osb")
-            nc.scalar.copy(out=osb[:], in_=ob[:])
-            nc.sync.dma_start(out=out[CB * c:CB * (c + 1)].rearrange("n i j -> i n j"), in_=osb[:])
+            if vector:
+                nc.vector.tensor_copy(out=osb[:, lo:hi, :], in_=ob[:, lo:hi, :])
+            else:
+                nc.scalar.copy(out=osb[:, lo:hi, :], in_=ob[:, lo:hi, :])
+            nc.sync.dma_start(out=out[CB * c + lo:CB * c + hi].rearrange("n i j -> i n j"), in_=osb[:, lo:hi, :])
 
-        load_l(0)
+        load_l(0, 0, 8)
         load_h(0, 0, 8)
+        load_l(0, 8, GB)
         load_h(0, 8, 16)
         for c8 in range(8):
             nc.sync.dma_start(out=wraw[c8:P:8, :, :], in_=wv[c8])
         load_h(0, 16, 32)
-        load_l(1)
+        load_l(1, 0, GB)
+        load_h(1, 0, 32)
         y_copy(0, 0)
         l_direct(0, 2)
         h_banks(0, 0)
@@ -271,25 +286,38 @@ def tile_qriaffine_t_kernel(tc, layer1, layer2, layer3, h1, h2, h3, W, out):
         l_direct(0, 1)
         y_copy(0, 1)
         h_banks(0, 1)
-        l_prep(0)
         for s in (2, 0, 1):
             l_direct(1, s)
-        l_load(1)
-        load_h(1, 0, 32)
         y_copy(1, 0)
         for g in range(2):
             for u in range(2):
                 for e in range(2):
                     nc.gpsimd.tensor_scalar(out=wo[:, g, u, e], in0=wr[:, g, u, e], scalar1=1.0, scalar2=0.0, op0=MULT, op1=ADD)
+        for c in (2, 3):
+            for s in (2, 0, 1):
+                l_direct(c, s)
 
-        for c in range(NCH + 4):
+        last = NCH - 1
+        for c in range(NCH + 1):
             if (c + 6) % 4 == 0 and 2 <= (c + 6) // 4 < NG:
-                load_l((c + 6) // 4)
+                load_l((c + 6) // 4, 0, GB)
                 load_h((c + 6) // 4, 0, 32)
             if (c + 3) % 4 == 0 and (c + 3) // 4 < NG:
                 l_prep((c + 3) // 4)
             if c == 1:
                 nc.vector.quantize_mx(out=wq[:].bitcast(FP8X4), scales=ws[:], in_=win[:])
+            if c == last + 1:
+                mm1(last, (4, 5))
+                quant(last, "r_in", 1024, "rq", "rs")
+                mm1(last, (6, 7))
+                mm2(last - 2)
+                quant(last - 1, "q_in", 1024, "qq", "qs")
+                mm2(last - 1)
+                quant_q_half(last, 0)
+                mm2(last, 0, 2)
+                quant_q_half(last, 1)
+                mm2(last, 2, CB, True)
+                break
             prod_p(c, 0)
             if c == 1:
                 mm1(0, (0, 1, 2, 3))
@@ -299,14 +327,18 @@ def tile_qriaffine_t_kernel(tc, layer1, layer2, layer3, h1, h2, h3, W, out):
             mm1(c - 1, (6, 7))
             y_copy(c + 1, 1)
             y_copy(c + 2, 0)
+            if c == last:
+                quant(c, "p_in", 512, "pq", "ps")
+                mm1(c, (0, 1, 2))
             quant(c - 1, "r_in", 1024, "rq", "rs")
             prod_r(c, 0)
-            quant(c, "p_in", 512, "pq", "ps")
-            if c > 0:
-                mm1(c, (0, 1, 2))
+            if c != last:
+                quant(c, "p_in", 512, "pq", "ps")
+                if c > 0:
+                    mm1(c, (0, 1, 2))
             mm2(c - 3)
             prod_r(c, 1)
-            if ok(c) and c % 2 == 1:
+            if c % 2 == 1:
                 l_load((c + 1) // 2 + 1)
             h_banks(c + 1, 1)
             if c > 0:

@@ -36,6 +36,7 @@ def tile_qriaffine_t_kernel(tc, layer1, layer2, layer3, h1, h2, h3, W, out):
         lpp = ctx.enter_context(tc.tile_pool(name="lpp", bufs=2))
         zp = ctx.enter_context(tc.tile_pool(name="zp", bufs=6))
         yp = ctx.enter_context(tc.tile_pool(name="yp", bufs=2))
+        hcp = ctx.enter_context(tc.tile_pool(name="hcp", bufs=3))
         lrp = ctx.enter_context(tc.tile_pool(name="lrp", bufs=3))
         work = ctx.enter_context(tc.tile_pool(name="work", bufs=3))
         outp = ctx.enter_context(tc.tile_pool(name="outp", bufs=5))
@@ -47,6 +48,9 @@ def tile_qriaffine_t_kernel(tc, layer1, layer2, layer3, h1, h2, h3, W, out):
         make_identity(nc, ident_f[:])
         ident_b = const.tile([P, P], BF16, name="ident_b")
         make_identity(nc, ident_b[:])
+
+        sel = const.tile([P, 16, 16, 8], BF16, name="sel")
+        nc.vector.tensor_copy(out=sel[:], in_=ident_b[:].rearrange("p (u q) -> p u q", u=16).unsqueeze(2).to_broadcast([P, 16, 16, 8]))
 
         lv2 = layer2.rearrange("n j b -> j n b")
         lv1 = layer1.rearrange("n j b -> j n b")
@@ -168,8 +172,30 @@ def tile_qriaffine_t_kernel(tc, layer1, layer2, layer3, h1, h2, h3, W, out):
                 nc.vector.tensor_copy(out=y[:], in_=src.bitcast(I32).unsqueeze(2).to_broadcast([P, 2 * CB, 16, 8]))
             ys[(c, h)] = y
 
+        hcs = {}
+
+        def hc_prep(o):
+            if not 0 <= o < NUN:
+                return
+            g, half = o // 2, o % 2
+            hcb = ps_q.tile([P, P], F32, name="hcb", tag="qb")
+            nc.tensor.transpose(hcb[:], hw[(1, g)][:].rearrange("p k w -> p (k w)").bitcast(F32)[:, P * half:P * (half + 1)], ident_f[:])
+            hc = hcp.tile([P, P], F32, name="hc")
+            nc.scalar.copy(out=hc[:], in_=hcb[:])
+            hcs[o] = hc
+
         def h_banks(c, h):
             if not ok(c):
+                return
+            if h == 1 and c > 0:
+                hc = hcs[c // 2]
+                for pr in range(2):
+                    hb = ps_h.tile([P, 4, 2 * P], BF16, name="hbb", tag="hb")
+                    for i in range(4):
+                        unit = 8 * (c % 2) + 4 * pr + i
+                        nc.tensor.matmul(out=hb[:, i, :], lhsT=sel[:, unit].rearrange("p b q -> p (b q)"),
+                                         rhs=hc[:].bitcast(BF16), start=True, stop=True)
+                    hbs[(c, h, pr)] = hb
                 return
             y = ys[(c, h)]
             for pr in range(2):
@@ -202,7 +228,8 @@ def tile_qriaffine_t_kernel(tc, layer1, layer2, layer3, h1, h2, h3, W, out):
             shape = [P, 2, 2, P, 2, 2]
             nc.vector.tensor_tensor(
                 out=st[c]["r_in"][:, 2048 * pr:2048 * (pr + 1)].rearrange("p (n g j u e) -> p n g j u e", n=2, g=2, j=P, u=2, e=2),
-                in0=hbs[(c, 1, pr)][:].rearrange("p k x -> p (k x)").bitcast(BF16)
+                in0=(hbs[(c, 1, pr)][:].rearrange("p k x -> p (k x)").bitcast(BF16) if c == 0
+                     else hbs[(c, 1, pr)][:].rearrange("p k x -> p (k x)"))
                 .rearrange("p (n j u e) -> p n j u e", n=2, j=P, u=2, e=2).unsqueeze(2).to_broadcast(shape),
                 in1=lrep2[c // 2][:, 2 * P * nl:2 * P * (nl + 2)].bitcast(BF16)
                 .rearrange("p (n g j e) -> p n g j e", n=2, g=2, j=P, e=2).unsqueeze(4).to_broadcast(shape),
@@ -288,6 +315,7 @@ def tile_qriaffine_t_kernel(tc, layer1, layer2, layer3, h1, h2, h3, W, out):
         h_banks(0, 1)
         for s in (2, 0, 1):
             l_direct(1, s)
+        hc_prep(0)
         y_copy(1, 0)
         for g in range(2):
             for u in range(2):
@@ -325,7 +353,8 @@ def tile_qriaffine_t_kernel(tc, layer1, layer2, layer3, h1, h2, h3, W, out):
             prod_p(c, 1)
             h_banks(c + 1, 0)
             mm1(c - 1, (6, 7))
-            y_copy(c + 1, 1)
+            if c % 2 == 0:
+                hc_prep(c // 2 + 1)
             y_copy(c + 2, 0)
             if c == last:
                 quant(c, "p_in", 512, "pq", "ps")

@@ -88,14 +88,20 @@ def tile_qriaffine_t_kernel(tc, layer1, layer2, layer3, h1, h2, h3, W, out):
             lo = LS_BASE + g * LS_WORDS + L2_WORDS
             return flat[lo:lo + L1_WORDS]
 
-        def l_prep(g):
+        lps = {}
+
+        def l_reorder(g):
             lp = lpp.tile([P, 48, GB], BF16, name="lp")
+            lps[g] = lp
             nc.gpsimd.memset(lp[:, 31, :], 1.0)
             nc.gpsimd.memset(lp[:, 47, :], 1.0)
             nc.gpsimd.tensor_scalar(out=lp[:, 0:31, :], in0=lraw2[g][:, :, 0:31].rearrange("p n b -> p b n"),
                                     scalar1=1.0, scalar2=0.0, op0=MULT, op1=ADD)
             nc.gpsimd.tensor_scalar(out=lp[:, 32:47, :], in0=lraw1[g][:, :, 0:15].rearrange("p n b -> p b n"),
                                     scalar1=1.0, scalar2=0.0, op0=MULT, op1=ADD)
+
+        def l_prep(g):
+            lp = lps[g]
             lt = ps_q.tile([P, 6, P], BF16, name="lt", tag="qb")
             for o in range(6):
                 nc.tensor.transpose(lt[:, o, :], lp[:, 8 * o:8 * o + 8, :].rearrange("p b n -> p (b n)"), ident_b[:])
@@ -331,7 +337,7 @@ def tile_qriaffine_t_kernel(tc, layer1, layer2, layer3, h1, h2, h3, W, out):
                 load_l((c + 6) // 4, 0, GB)
                 load_h((c + 6) // 4, 0, 32)
             if (c + 3) % 4 == 0 and (c + 3) // 4 < NG:
-                l_prep((c + 3) // 4)
+                l_reorder((c + 3) // 4)
             if c == 1:
                 nc.vector.quantize_mx(out=wq[:].bitcast(FP8X4), scales=ws[:], in_=win[:])
             if c == last + 1:
@@ -353,6 +359,8 @@ def tile_qriaffine_t_kernel(tc, layer1, layer2, layer3, h1, h2, h3, W, out):
             prod_p(c, 1)
             h_banks(c + 1, 0)
             mm1(c - 1, (6, 7))
+            if (c + 3) % 4 == 0 and (c + 3) // 4 < NG:
+                l_prep((c + 3) // 4)
             if c % 2 == 0:
                 hc_prep(c // 2 + 1)
             y_copy(c + 2, 0)

@@ -88,20 +88,20 @@ def tile_qriaffine_t_kernel(tc, layer1, layer2, layer3, h1, h2, h3, W, out):
             lo = LS_BASE + g * LS_WORDS + L2_WORDS
             return flat[lo:lo + L1_WORDS]
 
-        lps = {}
-
-        def l_reorder(g):
-            lp = lpp.tile([P, 48, GB], BF16, name="lp")
-            lps[g] = lp
-            nc.gpsimd.memset(lp[:, 31, :], 1.0)
-            nc.gpsimd.memset(lp[:, 47, :], 1.0)
-            nc.gpsimd.tensor_scalar(out=lp[:, 0:31, :], in0=lraw2[g][:, :, 0:31].rearrange("p n b -> p b n"),
-                                    scalar1=1.0, scalar2=0.0, op0=MULT, op1=ADD)
-            nc.gpsimd.tensor_scalar(out=lp[:, 32:47, :], in0=lraw1[g][:, :, 0:15].rearrange("p n b -> p b n"),
-                                    scalar1=1.0, scalar2=0.0, op0=MULT, op1=ADD)
-
         def l_prep(g):
-            lp = lps[g]
+            lp = lpp.tile([P, 48, GB], BF16, name="lp")
+            if g == 1:
+                nc.vector.memset(lp[:, 31, :], 1.0)
+                nc.vector.memset(lp[:, 47, :], 1.0)
+                nc.vector.tensor_copy(out=lp[:, 0:31, :], in_=lraw2[g][:, :, 0:31].rearrange("p n b -> p b n"))
+                nc.vector.tensor_copy(out=lp[:, 32:47, :], in_=lraw1[g][:, :, 0:15].rearrange("p n b -> p b n"))
+            else:
+                nc.gpsimd.memset(lp[:, 31, :], 1.0)
+                nc.gpsimd.memset(lp[:, 47, :], 1.0)
+                nc.gpsimd.tensor_scalar(out=lp[:, 0:31, :], in0=lraw2[g][:, :, 0:31].rearrange("p n b -> p b n"),
+                                        scalar1=1.0, scalar2=0.0, op0=MULT, op1=ADD)
+                nc.gpsimd.tensor_scalar(out=lp[:, 32:47, :], in0=lraw1[g][:, :, 0:15].rearrange("p n b -> p b n"),
+                                        scalar1=1.0, scalar2=0.0, op0=MULT, op1=ADD)
             lt = ps_q.tile([P, 6, P], BF16, name="lt", tag="qb")
             for o in range(6):
                 nc.tensor.transpose(lt[:, o, :], lp[:, 8 * o:8 * o + 8, :].rearrange("p b n -> p (b n)"), ident_b[:])
@@ -336,8 +336,11 @@ def tile_qriaffine_t_kernel(tc, layer1, layer2, layer3, h1, h2, h3, W, out):
             if (c + 6) % 4 == 0 and 2 <= (c + 6) // 4 < NG:
                 load_l((c + 6) // 4, 0, GB)
                 load_h((c + 6) // 4, 0, 32)
-            if (c + 3) % 4 == 0 and (c + 3) // 4 < NG:
-                l_reorder((c + 3) // 4)
+            if c == 1:
+                l_prep(1)
+                l_load(2)
+            if c % 4 == 0 and 2 <= c // 4 + 1 < NG:
+                l_prep(c // 4 + 1)
             if c == 1:
                 nc.vector.quantize_mx(out=wq[:].bitcast(FP8X4), scales=ws[:], in_=win[:])
             if c == last + 1:
@@ -359,8 +362,6 @@ def tile_qriaffine_t_kernel(tc, layer1, layer2, layer3, h1, h2, h3, W, out):
             prod_p(c, 1)
             h_banks(c + 1, 0)
             mm1(c - 1, (6, 7))
-            if (c + 3) % 4 == 0 and (c + 3) // 4 < NG:
-                l_prep((c + 3) // 4)
             if c % 2 == 0:
                 hc_prep(c // 2 + 1)
             y_copy(c + 2, 0)
@@ -375,8 +376,8 @@ def tile_qriaffine_t_kernel(tc, layer1, layer2, layer3, h1, h2, h3, W, out):
                     mm1(c, (0, 1, 2))
             mm2(c - 3)
             prod_r(c, 1)
-            if c % 2 == 1:
-                l_load((c + 1) // 2 + 1)
+            if c % 2 == 0 and c >= 2:
+                l_load(c // 2 + 2)
             h_banks(c + 1, 1)
             if c > 0:
                 mm1(c, (3,))

@@ -55,8 +55,8 @@ def tile_qriaffine_t_kernel(tc, layer1, layer2, layer3, h1, h2, h3, W, out):
         lv2 = layer2.rearrange("n j b -> j n b")
         lv1 = layer1.rearrange("n j b -> j n b")
         hv = [
-            h1.rearrange("n (a j) (u w) -> (j u) (n a) w", a=2, u=2),
-            h2.rearrange("n (a j) (u w) -> (j u) (n a) w", a=2, u=2),
+            h1.rearrange("n j w -> j n w"),
+            h2.rearrange("n j w -> j n w"),
         ]
         lraw2 = {}
         lraw1 = {}
@@ -75,8 +75,8 @@ def tile_qriaffine_t_kernel(tc, layer1, layer2, layer3, h1, h2, h3, W, out):
         def load_h(g, lo, hi):
             for h in range(2):
                 if (h, g) not in hw:
-                    hw[(h, g)] = inp.tile([P, 2 * GB, 16], BF16, name="hw%d_%d" % (h, g))
-                nc.sync.dma_start(out=hw[(h, g)][:, lo:hi, :], in_=hv[h][:, 2 * GB * g + lo:2 * GB * g + hi, :])
+                    hw[(h, g)] = inp.tile([P, GB, 32], BF16, name="hw%d_%d" % (h, g))
+                nc.sync.dma_start(out=hw[(h, g)][:, lo:hi, :], in_=hv[h][:, GB * g + lo:GB * g + hi, :])
 
         flat = out.rearrange("n i j -> (n i j)")
 
@@ -108,7 +108,7 @@ def tile_qriaffine_t_kernel(tc, layer1, layer2, layer3, h1, h2, h3, W, out):
             lc = lpp.tile([P, 6, P, 2], BF16, name="lc")
             nc.scalar.copy(out=lc[:], in_=lt[:].unsqueeze(3).to_broadcast([P, 6, P, 2]))
             lcw = lc[:].rearrange("p o j e -> p o (j e)").bitcast(F32)
-            d2 = scratch2(g).rearrange("(xh b n g w) -> g (b n) xh w", xh=2, b=8, n=GB, g=2, w=P)
+            d2 = scratch2(g).rearrange("(g xh b n w) -> g (b n) xh w", xh=2, b=8, n=GB, g=2, w=P)
             for gg in range(2):
                 nc.sync.dma_start(out=d2[gg], in_=lcw[:, 2 * gg:2 * gg + 2, :])
             nc.sync.dma_start(out=scratch1(g).rearrange("(xh b n w) -> (b n) xh w", xh=2, b=8, n=GB, w=P), in_=lcw[:, 4:6, :])
@@ -126,11 +126,11 @@ def tile_qriaffine_t_kernel(tc, layer1, layer2, layer3, h1, h2, h3, W, out):
                 return
             g, half = un // 2, un % 2
             l_tiles(un)
-            s2 = scratch2(g).rearrange("(x m) -> x m", x=16)[:, 2048 * half:2048 * (half + 1)]
+            s2 = scratch2(g).rearrange("(g x m) -> x g m", g=2, x=16)[:, :, 1024 * half:1024 * (half + 1)]
             s1 = scratch1(g).rearrange("(x m) -> x m", x=16)[:, 1024 * half:1024 * (half + 1)]
             for r in (0, 4, 1, 5, 2, 6, 3, 7):
                 nc.sync.dma_start(out=lrep1[un][r:P:8, :], in_=s1)
-                nc.sync.dma_start(out=lrep2[un][r:P:8, :], in_=s2)
+                nc.sync.dma_start(out=lrep2[un][r:P:8, :].rearrange("p (g m) -> p g m", g=2), in_=s2)
 
         def l_direct(c, s):
             un = c // 2
@@ -150,8 +150,8 @@ def tile_qriaffine_t_kernel(tc, layer1, layer2, layer3, h1, h2, h3, W, out):
             if s == 2:
                 nc.scalar.copy(out=lrep1[un][:, P * m0:P * (m0 + CB)].rearrange("p (n j) -> p n j", n=CB), in_=zb[:])
             else:
-                dst = lrep2[un][:].rearrange("p (n g j) -> p n g j", n=UB, g=2, j=P)
-                nc.scalar.copy(out=dst[:, m0:m0 + CB, s, :], in_=zb[:])
+                dst = lrep2[un][:].rearrange("p (g n j) -> p g n j", n=UB, g=2, j=P)
+                nc.scalar.copy(out=dst[:, s, m0:m0 + CB, :], in_=zb[:])
 
         wv = W.rearrange("a b (u c e) d -> c a (b u) (e d)", u=2, c=8, e=2)
         wraw = const.tile([P, 64, 64], BF16, name="wraw")
@@ -171,7 +171,7 @@ def tile_qriaffine_t_kernel(tc, layer1, layer2, layer3, h1, h2, h3, W, out):
                 return
             g, c4 = c // 4, c % 4
             y = yp.tile([P, 2 * CB, 16, 8], I32, name="y%d" % h)
-            src = hw[(h, g)][:, 2 * CB * c4:2 * CB * (c4 + 1), :]
+            src = hw[(h, g)][:, CB * c4:CB * (c4 + 1), :].rearrange("p n (u w) -> p (n u) w", u=2)
             if h == 0:
                 nc.scalar.copy(out=y[:].bitcast(F32), in_=src.bitcast(F32).unsqueeze(2).to_broadcast([P, 2 * CB, 16, 8]))
             else:
@@ -198,7 +198,7 @@ def tile_qriaffine_t_kernel(tc, layer1, layer2, layer3, h1, h2, h3, W, out):
                 for pr in range(2):
                     hb = ps_h.tile([P, 4, 2 * P], BF16, name="hbb", tag="hb")
                     for i in range(4):
-                        unit = 8 * (c % 2) + 4 * pr + i
+                        unit = 8 * (c % 2) + 4 * pr + 2 * (i % 2) + i // 2
                         nc.tensor.matmul(out=hb[:, i, :], lhsT=sel[:, unit].rearrange("p b q -> p (b q)"),
                                          rhs=hc[:].bitcast(BF16), start=True, stop=True)
                     hbs[(c, h, pr)] = hb
@@ -207,7 +207,7 @@ def tile_qriaffine_t_kernel(tc, layer1, layer2, layer3, h1, h2, h3, W, out):
             for pr in range(2):
                 hb = ps_h.tile([P, 4, P], F32, name="hb")
                 for i in range(4):
-                    nc.tensor.transpose(hb[:, i, :], y[:, 4 * pr + i].rearrange("p b q -> p (b q)").bitcast(F32), ident_f[:])
+                    nc.tensor.transpose(hb[:, i, :], y[:, 4 * pr + 2 * (i % 2) + i // 2].rearrange("p b q -> p (b q)").bitcast(F32), ident_f[:])
                 hbs[(c, h, pr)] = hb
 
         def prod_p(c, pr):
@@ -220,7 +220,7 @@ def tile_qriaffine_t_kernel(tc, layer1, layer2, layer3, h1, h2, h3, W, out):
             nl = CB * (c % 2) + 2 * pr
             nc.vector.tensor_tensor(
                 out=st[c]["p_in"][:, 1024 * pr:1024 * (pr + 1)].rearrange("p (c u e) -> p c u e", u=2, e=2),
-                in0=hbs[(c, 0, pr)][:].rearrange("p k x -> p (k x)").bitcast(BF16).rearrange("p (c u e) -> p c u e", u=2, e=2),
+                in0=hbs[(c, 0, pr)][:].rearrange("p k x -> p (k x)").bitcast(BF16).rearrange("p (u c e) -> p c u e", u=2, e=2),
                 in1=lrep1[c // 2][:, P * nl:P * (nl + 2)].bitcast(BF16).rearrange("p (c e) -> p c e", e=2)
                 .unsqueeze(2).to_broadcast([P, 256, 2, 2]),
                 op=MULT)
@@ -231,15 +231,17 @@ def tile_qriaffine_t_kernel(tc, layer1, layer2, layer3, h1, h2, h3, W, out):
             if pr == 0:
                 st[c]["r_in"] = work.tile([P, 4096], BF16, name="r_in", align_bytes=64)
             nl = CB * (c % 2) + 2 * pr
-            shape = [P, 2, 2, P, 2, 2]
-            nc.vector.tensor_tensor(
-                out=st[c]["r_in"][:, 2048 * pr:2048 * (pr + 1)].rearrange("p (n g j u e) -> p n g j u e", n=2, g=2, j=P, u=2, e=2),
-                in0=(hbs[(c, 1, pr)][:].rearrange("p k x -> p (k x)").bitcast(BF16) if c == 0
-                     else hbs[(c, 1, pr)][:].rearrange("p k x -> p (k x)"))
-                .rearrange("p (n j u e) -> p n j u e", n=2, j=P, u=2, e=2).unsqueeze(2).to_broadcast(shape),
-                in1=lrep2[c // 2][:, 2 * P * nl:2 * P * (nl + 2)].bitcast(BF16)
-                .rearrange("p (n g j e) -> p n g j e", n=2, g=2, j=P, e=2).unsqueeze(4).to_broadcast(shape),
-                op=MULT)
+            hb = hbs[(c, 1, pr)][:].rearrange("p k x -> p (k x)")
+            if c == 0:
+                hb = hb.bitcast(BF16)
+            for g in range(2):
+                lo = 1024 * (2 * pr + g)
+                nc.vector.tensor_tensor(
+                    out=st[c]["r_in"][:, lo:lo + 1024].rearrange("p (c u e) -> p c u e", u=2, e=2),
+                    in0=hb.rearrange("p (u c e) -> p c u e", u=2, e=2),
+                    in1=lrep2[c // 2][:, P * (UB * g + nl):P * (UB * g + nl + 2)].bitcast(BF16).rearrange("p (c e) -> p c e", e=2)
+                    .unsqueeze(2).to_broadcast([P, 256, 2, 2]),
+                    op=MULT)
 
         def quant(c, key, words, codes, scales):
             if not ok(c):
@@ -291,10 +293,11 @@ def tile_qriaffine_t_kernel(tc, layer1, layer2, layer3, h1, h2, h3, W, out):
             for n in range(lo, hi):
                 for g in range(2):
                     a = (2 * n + g) * P
+                    b = (4 * (n // 2) + 2 * g + n % 2) * P
                     nc.tensor.matmul_mx(
                         out=ob[:, n, :],
                         lhsT=s["qq"][:, a:a + P].bitcast(FP8X4), lhsT_scale=s["qs"][:, a:a + P],
-                        rhs=s["rq"][:, a:a + P].bitcast(FP8X4), rhs_scale=s["rs"][:, a:a + P],
+                        rhs=s["rq"][:, b:b + P].bitcast(FP8X4), rhs_scale=s["rs"][:, b:b + P],
                         start=(g == 0), stop=(g == 1))
             osb = outp.tile([P, CB, P], F32, name="osb")
             if vector:
@@ -304,14 +307,14 @@ def tile_qriaffine_t_kernel(tc, layer1, layer2, layer3, h1, h2, h3, W, out):
             nc.sync.dma_start(out=out[CB * c + lo:CB * c + hi].rearrange("n i j -> i n j"), in_=osb[:, lo:hi, :])
 
         load_l(0, 0, 8)
-        load_h(0, 0, 8)
+        load_h(0, 0, 4)
         load_l(0, 8, GB)
-        load_h(0, 8, 16)
+        load_h(0, 4, 8)
         for c8 in range(8):
             nc.sync.dma_start(out=wraw[c8:P:8, :, :], in_=wv[c8])
-        load_h(0, 16, 32)
+        load_h(0, 8, GB)
         load_l(1, 0, GB)
-        load_h(1, 0, 32)
+        load_h(1, 0, GB)
         y_copy(0, 0)
         l_direct(0, 2)
         h_banks(0, 0)
@@ -335,7 +338,7 @@ def tile_qriaffine_t_kernel(tc, layer1, layer2, layer3, h1, h2, h3, W, out):
         for c in range(NCH + 1):
             if (c + 6) % 4 == 0 and 2 <= (c + 6) // 4 < NG:
                 load_l((c + 6) // 4, 0, GB)
-                load_h((c + 6) // 4, 0, 32)
+                load_h((c + 6) // 4, 0, GB)
             if c == 1:
                 l_prep(1)
                 l_load(2)

@@ -7,7 +7,6 @@ F32 = mybir.dt.float32
 BF16 = mybir.dt.bfloat16
 U8 = mybir.dt.uint8
 U32 = mybir.dt.uint32
-I32 = mybir.dt.int32
 FP8X4 = mybir.dt.float8_e4m3fn_x4
 MULT = mybir.AluOpType.mult
 ADD = mybir.AluOpType.add
@@ -20,11 +19,10 @@ GB = 16
 NG = NB // GB
 UB = 8
 NUN = NB // UB
+LEAD = 6
 FLOPS = 2 * 8192 * 512 * 1024 + 2 * 64 * 128 * 128 * 1024
 
-L2_WORDS = 16 * GB * 2 * 128
-L1_WORDS = 16 * GB * 128
-LS_WORDS = L2_WORDS + L1_WORDS
+LS_WORDS = 16 * GB * 2 * P
 LS_BASE = NB * P * P - NG * LS_WORDS
 
 
@@ -34,14 +32,13 @@ def tile_qriaffine_t_kernel(tc, layer1, layer2, layer3, h1, h2, h3, W, out):
         const = ctx.enter_context(tc.tile_pool(name="const", bufs=1))
         inp = ctx.enter_context(tc.tile_pool(name="inp", bufs=1))
         lpp = ctx.enter_context(tc.tile_pool(name="lpp", bufs=2))
-        zp = ctx.enter_context(tc.tile_pool(name="zp", bufs=6))
-        yp = ctx.enter_context(tc.tile_pool(name="yp", bufs=2))
+        zp = ctx.enter_context(tc.tile_pool(name="zp", bufs=2))
         hcp = ctx.enter_context(tc.tile_pool(name="hcp", bufs=3))
         lrp = ctx.enter_context(tc.tile_pool(name="lrp", bufs=3))
         work = ctx.enter_context(tc.tile_pool(name="work", bufs=3))
         outp = ctx.enter_context(tc.tile_pool(name="outp", bufs=5))
-        ps_h = ctx.enter_context(tc.psum_pool(name="ps_h", bufs=4))
-        ps_q = ctx.enter_context(tc.psum_pool(name="ps_q", bufs=4))
+        ps_h = ctx.enter_context(tc.psum_pool(name="ps_h", bufs=2))
+        ps_q = ctx.enter_context(tc.psum_pool(name="ps_q", bufs=3))
         ctx.enter_context(tc.manual_schedule())
 
         ident_f = const.tile([P, P], F32, name="ident_f")
@@ -52,132 +49,104 @@ def tile_qriaffine_t_kernel(tc, layer1, layer2, layer3, h1, h2, h3, W, out):
         sel = const.tile([P, 16, 16, 8], BF16, name="sel")
         nc.vector.tensor_copy(out=sel[:], in_=ident_b[:].rearrange("p (u q) -> p u q", u=16).unsqueeze(2).to_broadcast([P, 16, 16, 8]))
 
-        lv2 = layer2.rearrange("n j b -> j n b")
-        lv1 = layer1.rearrange("n j b -> j n b")
-        hv = [
-            h1.rearrange("n j w -> j n w"),
-            h2.rearrange("n j w -> j n w"),
-        ]
         lraw2 = {}
         lraw1 = {}
-        hw = {}
+        l1d = {}
 
         def ok(c):
             return 0 <= c < NCH
 
-        def load_l(g, lo, hi):
-            if g not in lraw2:
-                lraw2[g] = inp.tile([P, GB, 32], BF16, name="lraw2_%d" % g)
-                lraw1[g] = inp.tile([P, GB, 16], BF16, name="lraw1_%d" % g)
-            nc.sync.dma_start(out=lraw1[g][:, lo:hi, 0:15], in_=lv1[:, GB * g + lo:GB * g + hi, :])
-            nc.sync.dma_start(out=lraw2[g][:, lo:hi, 0:31], in_=lv2[:, GB * g + lo:GB * g + hi, :])
+        def load(into, src, width, cols, g, lo, hi, name):
+            if g not in into:
+                into[g] = inp.tile([P, GB, width], BF16, name="%s_%d" % (name, g))
+            nc.sync.dma_start(out=into[g][:, lo:hi, 0:cols], in_=src.rearrange("n j w -> j n w")[:, GB * g + lo:GB * g + hi, :])
 
-        def load_h(g, lo, hi):
-            for h in range(2):
-                if (h, g) not in hw:
-                    hw[(h, g)] = inp.tile([P, GB, 32], BF16, name="hw%d_%d" % (h, g))
-                nc.sync.dma_start(out=hw[(h, g)][:, lo:hi, :], in_=hv[h][:, GB * g + lo:GB * g + hi, :])
+        hw1 = {}
+        hw2 = {}
+
+        def load_p(g, lo, hi):
+            load(lraw1, layer1, 16, 15, g, lo, hi, "lraw1")
+            load(hw1, h1, 32, 32, g, lo, hi, "hw1")
+
+        def load_r(g, lo, hi):
+            load(lraw2, layer2, 32, 31, g, lo, hi, "lraw2")
+            load(hw2, h2, 32, 32, g, lo, hi, "hw2")
+
+        def l1_dup(g, lo, hi, eng):
+            if g not in l1d:
+                l1d[g] = inp.tile([P, GB // CB, 16, CB, 2], BF16, name="l1d_%d" % g)
+            k0, k1 = lo // CB, hi // CB
+            eng.memset(l1d[g][:, k0:k1, 15, :, :], 1.0)
+            src = lraw1[g][:, lo:hi, 0:15].rearrange("p (k n) a -> p a k n", n=CB).unsqueeze(4).to_broadcast([P, 15, k1 - k0, CB, 2])
+            dst = l1d[g][:, k0:k1, 0:15].rearrange("p k a n e -> p a k n e")
+            if eng is nc.vector:
+                eng.tensor_copy(out=dst, in_=src)
+            else:
+                eng.tensor_scalar(out=dst, in0=src, scalar1=1.0, scalar2=0.0, op0=MULT, op1=ADD)
 
         flat = out.rearrange("n i j -> (n i j)")
 
         def scratch2(g):
             lo = LS_BASE + g * LS_WORDS
-            return flat[lo:lo + L2_WORDS]
-
-        def scratch1(g):
-            lo = LS_BASE + g * LS_WORDS + L2_WORDS
-            return flat[lo:lo + L1_WORDS]
+            return flat[lo:lo + LS_WORDS]
 
         def l_prep(g):
-            lp = lpp.tile([P, 48, GB], BF16, name="lp")
-            if g == 1:
-                nc.vector.memset(lp[:, 31, :], 1.0)
-                nc.vector.memset(lp[:, 47, :], 1.0)
-                nc.vector.tensor_copy(out=lp[:, 0:31, :], in_=lraw2[g][:, :, 0:31].rearrange("p n b -> p b n"))
-                nc.vector.tensor_copy(out=lp[:, 32:47, :], in_=lraw1[g][:, :, 0:15].rearrange("p n b -> p b n"))
-            else:
-                nc.gpsimd.memset(lp[:, 31, :], 1.0)
-                nc.gpsimd.memset(lp[:, 47, :], 1.0)
-                nc.gpsimd.tensor_scalar(out=lp[:, 0:31, :], in0=lraw2[g][:, :, 0:31].rearrange("p n b -> p b n"),
-                                        scalar1=1.0, scalar2=0.0, op0=MULT, op1=ADD)
-                nc.gpsimd.tensor_scalar(out=lp[:, 32:47, :], in0=lraw1[g][:, :, 0:15].rearrange("p n b -> p b n"),
-                                        scalar1=1.0, scalar2=0.0, op0=MULT, op1=ADD)
-            lt = ps_q.tile([P, 6, P], BF16, name="lt", tag="qb")
-            for o in range(6):
-                nc.tensor.transpose(lt[:, o, :], lp[:, 8 * o:8 * o + 8, :].rearrange("p b n -> p (b n)"), ident_b[:])
-            lc = lpp.tile([P, 6, P, 2], BF16, name="lc")
-            nc.scalar.copy(out=lc[:], in_=lt[:].unsqueeze(3).to_broadcast([P, 6, P, 2]))
-            lcw = lc[:].rearrange("p o j e -> p o (j e)").bitcast(F32)
+            lp = lpp.tile([P, 32, GB, 2], BF16, name="lp")
+            nc.gpsimd.memset(lp[:, 31, :, :], 1.0)
+            nc.gpsimd.tensor_scalar(out=lp[:, 0:31, :, :], in0=lraw2[g][:, :, 0:31].rearrange("p n b -> p b n").unsqueeze(3).to_broadcast([P, 31, GB, 2]),
+                                    scalar1=1.0, scalar2=0.0, op0=MULT, op1=ADD)
+            lt = ps_q.tile([P, 4, P], F32, name="lt", tag="qb")
+            for o in range(4):
+                nc.tensor.transpose(lt[:, o, :], lp[:, 8 * o:8 * o + 8].rearrange("p b n e -> p (b n e)").bitcast(F32), ident_f[:])
+            lcw = lpp.tile([P, 4, P], F32, name="lcw")
+            nc.scalar.copy(out=lcw[:], in_=lt[:])
             d2 = scratch2(g).rearrange("(g xh b n w) -> g (b n) xh w", xh=2, b=8, n=GB, g=2, w=P)
             for gg in range(2):
                 nc.sync.dma_start(out=d2[gg], in_=lcw[:, 2 * gg:2 * gg + 2, :])
-            nc.sync.dma_start(out=scratch1(g).rearrange("(xh b n w) -> (b n) xh w", xh=2, b=8, n=GB, w=P), in_=lcw[:, 4:6, :])
 
         lrep2 = {}
-        lrep1 = {}
+        l0 = const.tile([P, 2 * CB * P], F32, name="l0")
+
+        def l2_words(c, g, n):
+            if c == 0:
+                return l0[:, P * (CB * g + n):P * (CB * g + n + 2)]
+            n += CB * (c % 2)
+            return lrep2[c // 2][:, P * (UB * g + n):P * (UB * g + n + 2)]
 
         def l_tiles(un):
             if un not in lrep2:
                 lrep2[un] = lrp.tile([P, UB * 2 * P], F32, name="lrep2")
-                lrep1[un] = lrp.tile([P, UB * P], F32, name="lrep1")
 
-        def l_load(un):
+        def l_load(un, lo=0, hi=UB):
             if not 0 <= un < NUN:
                 return
             g, half = un // 2, un % 2
             l_tiles(un)
-            s2 = scratch2(g).rearrange("(g x m) -> x g m", g=2, x=16)[:, :, 1024 * half:1024 * (half + 1)]
-            s1 = scratch1(g).rearrange("(x m) -> x m", x=16)[:, 1024 * half:1024 * (half + 1)]
+            s2 = scratch2(g).rearrange("(g x m) -> x g m", g=2, x=16)[:, :, P * (UB * half + lo):P * (UB * half + hi)]
             for r in (0, 4, 1, 5, 2, 6, 3, 7):
-                nc.sync.dma_start(out=lrep1[un][r:P:8, :], in_=s1)
-                nc.sync.dma_start(out=lrep2[un][r:P:8, :].rearrange("p (g m) -> p g m", g=2), in_=s2)
+                nc.sync.dma_start(out=lrep2[un][r:P:8, :].rearrange("p (g m) -> p g m", g=2)[:, :, P * lo:P * hi], in_=s2)
 
-        def l_direct(c, s):
-            un = c // 2
-            l_tiles(un)
+        def l_direct(s):
             z = zp.tile([P, CB, 16, 16], BF16, name="z")
-            n0 = CB * c
-            m0 = CB * (c % 2)
             if s == 0:
-                nc.vector.tensor_copy(out=z[:], in_=lraw2[0][:, n0:n0 + CB, 0:16].unsqueeze(3).to_broadcast([P, CB, 16, 16]))
+                nc.vector.tensor_copy(out=z[:], in_=lraw2[0][:, 0:CB, 0:16].unsqueeze(3).to_broadcast([P, CB, 16, 16]))
             else:
-                src = lraw2[0][:, n0:n0 + CB, 16:31] if s == 1 else lraw1[0][:, n0:n0 + CB, 0:15]
-                nc.vector.memset(z[:, :, 15, :], 1.0)
-                nc.vector.tensor_copy(out=z[:, :, 0:15, :], in_=src.unsqueeze(3).to_broadcast([P, CB, 15, 16]))
+                nc.gpsimd.memset(z[:, :, 15, :], 1.0)
+                nc.vector.tensor_copy(out=z[:, :, 0:15, :], in_=lraw2[0][:, 0:CB, 16:31].unsqueeze(3).to_broadcast([P, CB, 15, 16]))
             zb = ps_q.tile([P, CB, P], F32, name="zb", tag="qb")
             for n in range(CB):
                 nc.tensor.transpose(zb[:, n, :], z[:, n].rearrange("p x e -> p (x e)").bitcast(F32), ident_f[:])
-            if s == 2:
-                nc.scalar.copy(out=lrep1[un][:, P * m0:P * (m0 + CB)].rearrange("p (n j) -> p n j", n=CB), in_=zb[:])
-            else:
-                dst = lrep2[un][:].rearrange("p (g n j) -> p g n j", n=UB, g=2, j=P)
-                nc.scalar.copy(out=dst[:, s, m0:m0 + CB, :], in_=zb[:])
+            nc.scalar.copy(out=l0[:, CB * P * s:CB * P * (s + 1)].rearrange("p (n j) -> p n j", n=CB), in_=zb[:])
 
-        wv = W.rearrange("a b (u c e) d -> c a (b u) (e d)", u=2, c=8, e=2)
-        wraw = const.tile([P, 64, 64], BF16, name="wraw")
+        wv = W.rearrange("a b (q t) d -> q a b (t d)", t=4)
+        wraw = const.tile([P, 32, P], BF16, name="wraw")
         win = const.tile([P, 4096], BF16, name="win", align_bytes=64)
         wq = const.tile([P, 1024], U32, name="wq", align_bytes=64)
         ws = const.tile([P, 1024], U8, name="ws", align_bytes=64)
-        wr = wraw[:].rearrange("p x y -> p (x y)").rearrange(
-            "p (g b t u q e) -> p g u e b q t", g=2, b=16, t=4, u=2, q=8, e=2)
+        wr = wraw[:].rearrange("p b (t x) -> p b t x", t=4).rearrange("p (g b) t (u q e) -> p g u e b q t", g=2, u=2, e=2)
         wo = win[:].rearrange("p (g u e b q t) -> p g u e b q t", g=2, u=2, e=2, b=16, q=8, t=4)
 
-        ys = {}
-        hbs = {}
         st = {}
-
-        def y_copy(c, h):
-            if not ok(c):
-                return
-            g, c4 = c // 4, c % 4
-            y = yp.tile([P, 2 * CB, 16, 8], I32, name="y%d" % h)
-            src = hw[(h, g)][:, CB * c4:CB * (c4 + 1), :].rearrange("p n (u w) -> p (n u) w", u=2)
-            if h == 0:
-                nc.scalar.copy(out=y[:].bitcast(F32), in_=src.bitcast(F32).unsqueeze(2).to_broadcast([P, 2 * CB, 16, 8]))
-            else:
-                nc.vector.tensor_copy(out=y[:], in_=src.bitcast(I32).unsqueeze(2).to_broadcast([P, 2 * CB, 16, 8]))
-            ys[(c, h)] = y
-
         hcs = {}
 
         def hc_prep(o):
@@ -185,61 +154,60 @@ def tile_qriaffine_t_kernel(tc, layer1, layer2, layer3, h1, h2, h3, W, out):
                 return
             g, half = o // 2, o % 2
             hcb = ps_q.tile([P, P], F32, name="hcb", tag="qb")
-            nc.tensor.transpose(hcb[:], hw[(1, g)][:].rearrange("p k w -> p (k w)").bitcast(F32)[:, P * half:P * (half + 1)], ident_f[:])
+            nc.tensor.transpose(hcb[:], hw2[g][:].rearrange("p k w -> p (k w)").bitcast(F32)[:, P * half:P * (half + 1)], ident_f[:])
             hc = hcp.tile([P, P], F32, name="hc")
             nc.scalar.copy(out=hc[:], in_=hcb[:])
             hcs[o] = hc
 
-        def h_banks(c, h):
-            if not ok(c):
-                return
-            if h == 1 and c > 0:
-                hc = hcs[c // 2]
-                for pr in range(2):
-                    hb = ps_h.tile([P, 4, 2 * P], BF16, name="hbb", tag="hb")
-                    for i in range(4):
-                        unit = 8 * (c % 2) + 4 * pr + 2 * (i % 2) + i // 2
-                        nc.tensor.matmul(out=hb[:, i, :], lhsT=sel[:, unit].rearrange("p b q -> p (b q)"),
-                                         rhs=hc[:].bitcast(BF16), start=True, stop=True)
-                    hbs[(c, h, pr)] = hb
-                return
-            y = ys[(c, h)]
-            for pr in range(2):
-                hb = ps_h.tile([P, 4, P], F32, name="hb")
-                for i in range(4):
-                    nc.tensor.transpose(hb[:, i, :], y[:, 4 * pr + 2 * (i % 2) + i // 2].rearrange("p b q -> p (b q)").bitcast(F32), ident_f[:])
-                hbs[(c, h, pr)] = hb
+        hbs = {}
 
-        def prod_p(c, pr):
+        def h_bank(c, pr):
             if not ok(c):
                 return
-            if c not in st:
-                st[c] = {}
+            hb = ps_h.tile([P, 4, 2 * P], BF16, name="hb", bufs=3)
+            for i in range(4):
+                unit = 8 * (c % 2) + 4 * pr + 2 * (i % 2) + i // 2
+                nc.tensor.matmul(out=hb[:, i, :], lhsT=sel[:, unit].rearrange("p b q -> p (b q)"),
+                                 rhs=hcs[c // 2][:].bitcast(BF16), start=True, stop=True)
+            hbs[(c, pr)] = hb
+
+        def prod_p(c):
+            if not ok(c):
+                return
+            st[c] = {}
+            g, n0 = c // 4, CB * (c % 4)
+            pn = work.tile([P, 2, CB, 256], BF16, name="pn", bufs=2)
+            for u in range(2):
+                nc.vector.tensor_tensor(
+                    out=pn[:, u].rearrange("p n (a q e) -> p a n q e", a=16, e=2),
+                    in0=hw1[g][:, n0:n0 + CB].rearrange("p n (q v e) -> p n q v e", v=2, e=2)[:, :, :, u].unsqueeze(1).to_broadcast([P, 16, CB, 8, 2]),
+                    in1=l1d[g][:, c % 4].unsqueeze(3).to_broadcast([P, 16, CB, 8, 2]),
+                    op=MULT)
+            st[c]["pn"] = pn
+
+        def turn_p(c, pr):
+            if not ok(c):
+                return
             if pr == 0:
-                st[c]["p_in"] = work.tile([P, 2048], BF16, name="p_in", align_bytes=64)
-            nl = CB * (c % 2) + 2 * pr
-            nc.vector.tensor_tensor(
-                out=st[c]["p_in"][:, 1024 * pr:1024 * (pr + 1)].rearrange("p (c u e) -> p c u e", u=2, e=2),
-                in0=hbs[(c, 0, pr)][:].rearrange("p k x -> p (k x)").bitcast(BF16).rearrange("p (u c e) -> p c u e", u=2, e=2),
-                in1=lrep1[c // 2][:, P * nl:P * (nl + 2)].bitcast(BF16).rearrange("p (c e) -> p c e", e=2)
-                .unsqueeze(2).to_broadcast([P, 256, 2, 2]),
-                op=MULT)
+                st[c]["p_in"] = work.tile([P, 2048], BF16, name="p_in", align_bytes=64, bufs=2)
+            pt = ps_h.tile([P, 2, 2, P], F32, name="pt", bufs=2)
+            for n in range(2):
+                for u in range(2):
+                    nc.tensor.transpose(pt[:, n, u, :], st[c]["pn"][:, u, 2 * pr + n, :].bitcast(F32), ident_f[:])
+            nc.scalar.copy(out=st[c]["p_in"][:, 1024 * pr:1024 * (pr + 1)].bitcast(F32).rearrange("p (n i u) -> p n i u", n=2, u=2),
+                           in_=pt[:].rearrange("p n u i -> p n i u"))
 
         def prod_r(c, pr):
             if not ok(c):
                 return
             if pr == 0:
-                st[c]["r_in"] = work.tile([P, 4096], BF16, name="r_in", align_bytes=64)
-            nl = CB * (c % 2) + 2 * pr
-            hb = hbs[(c, 1, pr)][:].rearrange("p k x -> p (k x)")
-            if c == 0:
-                hb = hb.bitcast(BF16)
+                st[c]["r_in"] = work.tile([P, 4096], BF16, name="r_in", align_bytes=64, bufs=2)
             for g in range(2):
                 lo = 1024 * (2 * pr + g)
                 nc.vector.tensor_tensor(
                     out=st[c]["r_in"][:, lo:lo + 1024].rearrange("p (c u e) -> p c u e", u=2, e=2),
-                    in0=hb.rearrange("p (u c e) -> p c u e", u=2, e=2),
-                    in1=lrep2[c // 2][:, P * (UB * g + nl):P * (UB * g + nl + 2)].bitcast(BF16).rearrange("p (c e) -> p c e", e=2)
+                    in0=hbs[(c, pr)][:].rearrange("p k x -> p (k x)").rearrange("p (u c e) -> p c u e", u=2, e=2),
+                    in1=l2_words(c, g, 2 * pr).bitcast(BF16).rearrange("p (c e) -> p c e", e=2)
                     .unsqueeze(2).to_broadcast([P, 256, 2, 2]),
                     op=MULT)
 
@@ -251,8 +219,9 @@ def tile_qriaffine_t_kernel(tc, layer1, layer2, layer3, h1, h2, h3, W, out):
                 src = src[:].rearrange("p k x -> p (k x)")
             else:
                 src = src[:]
-            cd = work.tile([P, words], U32, name=codes, align_bytes=64)
-            sc = work.tile([P, words], U8, name=scales, align_bytes=64)
+            deep = LEAD + 2 if key == "p_in" else 3
+            cd = work.tile([P, words], U32, name=codes, align_bytes=64, bufs=deep)
+            sc = work.tile([P, words], U8, name=scales, align_bytes=64, bufs=deep)
             nc.vector.quantize_mx(out=cd[:].bitcast(FP8X4), scales=sc[:], in_=src)
             st[c][codes] = cd
             st[c][scales] = sc
@@ -285,7 +254,7 @@ def tile_qriaffine_t_kernel(tc, layer1, layer2, layer3, h1, h2, h3, W, out):
                 out=s["qq"][:, 512 * hf:512 * (hf + 1)].bitcast(FP8X4), scales=s["qs"][:, 512 * hf:512 * (hf + 1)],
                 in_=s["q_in"][:].rearrange("p k x -> p (k x)")[:, 2048 * hf:2048 * (hf + 1)])
 
-        def mm2(c, lo=0, hi=CB, vector=False):
+        def mm2(c, lo=0, hi=CB, vector=False, late=False):
             if not ok(c):
                 return
             s = st[c]
@@ -299,6 +268,14 @@ def tile_qriaffine_t_kernel(tc, layer1, layer2, layer3, h1, h2, h3, W, out):
                         lhsT=s["qq"][:, a:a + P].bitcast(FP8X4), lhsT_scale=s["qs"][:, a:a + P],
                         rhs=s["rq"][:, b:b + P].bitcast(FP8X4), rhs_scale=s["rs"][:, b:b + P],
                         start=(g == 0), stop=(g == 1))
+            st[c]["ob"] = ob
+            if not late:
+                store(c, lo, hi, vector)
+
+        def store(c, lo=0, hi=CB, vector=False):
+            if not ok(c):
+                return
+            ob = st[c]["ob"]
             osb = outp.tile([P, CB, P], F32, name="osb")
             if vector:
                 nc.vector.tensor_copy(out=osb[:, lo:hi, :], in_=ob[:, lo:hi, :])
@@ -306,82 +283,105 @@ def tile_qriaffine_t_kernel(tc, layer1, layer2, layer3, h1, h2, h3, W, out):
                 nc.scalar.copy(out=osb[:, lo:hi, :], in_=ob[:, lo:hi, :])
             nc.sync.dma_start(out=out[CB * c + lo:CB * c + hi].rearrange("n i j -> i n j"), in_=osb[:, lo:hi, :])
 
-        load_l(0, 0, 8)
-        load_h(0, 0, 4)
-        load_l(0, 8, GB)
-        load_h(0, 4, 8)
+        load_p(0, 0, 4)
+        load(lraw2, layer2, 32, 31, 0, 0, 8, "lraw2")
+        load_p(0, 4, 8)
+        load(hw2, h2, 32, 32, 0, 0, 8, "hw2")
         for c8 in range(8):
             nc.sync.dma_start(out=wraw[c8:P:8, :, :], in_=wv[c8])
-        load_h(0, 8, GB)
-        load_l(1, 0, GB)
-        load_h(1, 0, GB)
-        y_copy(0, 0)
-        l_direct(0, 2)
-        h_banks(0, 0)
-        l_direct(0, 0)
-        l_direct(0, 1)
-        y_copy(0, 1)
-        h_banks(0, 1)
-        for s in (2, 0, 1):
-            l_direct(1, s)
-        hc_prep(0)
-        y_copy(1, 0)
-        for g in range(2):
+        load(lraw2, layer2, 32, 31, 0, 8, GB, "lraw2")
+        load_p(0, 8, GB)
+        load(hw2, h2, 32, 32, 0, 8, GB, "hw2")
+        load_p(1, 0, GB)
+        load_r(1, 0, GB)
+
+        def w_part(g):
             for u in range(2):
                 for e in range(2):
-                    nc.gpsimd.tensor_scalar(out=wo[:, g, u, e], in0=wr[:, g, u, e], scalar1=1.0, scalar2=0.0, op0=MULT, op1=ADD)
-        for c in (2, 3):
-            for s in (2, 0, 1):
-                l_direct(c, s)
+                    nc.scalar.copy(out=wo[:, g, u, e], in_=wr[:, g, u, e])
+
+        def p_chunk(c):
+            prod_p(c)
+            turn_p(c, 0)
+            turn_p(c, 1)
+
+        l1_dup(0, 0, 4, nc.vector)
+        p_chunk(0)
+        l_direct(0)
+        l_direct(1)
+        l1_dup(0, 4, 8, nc.vector)
+        hc_prep(0)
+        p_chunk(1)
+        h_bank(0, 0)
+        h_bank(0, 1)
+        quant(0, "p_in", 512, "pq", "ps")
+        prod_r(0, 0)
+        w_part(0)
+        prod_r(0, 1)
+        quant(1, "p_in", 512, "pq", "ps")
+        w_part(1)
+        l_prep(0)
+        l_load(0, 4, 8)
+        l_load(1)
+        l1_dup(0, 8, GB, nc.vector)
+        prod_p(2)
+        quant(0, "r_in", 1024, "rq", "rs")
+        nc.vector.quantize_mx(out=wq[:].bitcast(FP8X4), scales=ws[:], in_=win[:])
+        turn_p(2, 0)
+        mm1(0, (0,))
+        turn_p(2, 1)
+        prod_p(3)
+        mm1(0, (1, 2, 3))
+        turn_p(3, 0)
+        quant(2, "p_in", 512, "pq", "ps")
+        mm1(0, (4, 5))
+        h_bank(1, 0)
+        turn_p(3, 1)
+        l1_dup(1, 0, GB, nc.gpsimd)
+        prod_p(4)
+        mm1(0, (6, 7))
+        quant(3, "p_in", 512, "pq", "ps")
+        turn_p(4, 0)
+        h_bank(1, 1)
+        turn_p(4, 1)
+        prod_p(5)
+        quant(4, "p_in", 512, "pq", "ps")
+        turn_p(5, 0)
+        turn_p(5, 1)
 
         last = NCH - 1
-        for c in range(NCH + 1):
-            if (c + 6) % 4 == 0 and 2 <= (c + 6) // 4 < NG:
-                load_l((c + 6) // 4, 0, GB)
-                load_h((c + 6) // 4, 0, GB)
-            if c == 1:
-                l_prep(1)
-                l_load(2)
-            if c % 4 == 0 and 2 <= c // 4 + 1 < NG:
+        for c in range(1, NCH):
+            if c in (1, 3):
+                load_p(c // 2 + 2, 0, GB)
+            if c in (2, 6):
+                load_r(c // 4 + 2, 0, GB)
+            if c % 4 == 1 and c // 4 + 1 < NG:
                 l_prep(c // 4 + 1)
-            if c == 1:
-                nc.vector.quantize_mx(out=wq[:].bitcast(FP8X4), scales=ws[:], in_=win[:])
-            if c == last + 1:
-                mm1(last, (4, 5))
-                quant(last, "r_in", 1024, "rq", "rs")
-                mm1(last, (6, 7))
-                mm2(last - 2)
-                quant(last - 1, "q_in", 1024, "qq", "qs")
-                mm2(last - 1)
-                quant_q_half(last, 0)
-                mm2(last, 0, 2)
-                quant_q_half(last, 1)
-                mm2(last, 2, CB, True)
-                break
-            prod_p(c, 0)
-            if c == 1:
-                mm1(0, (0, 1, 2, 3))
-            mm1(c - 1, (4, 5))
-            prod_p(c, 1)
-            h_banks(c + 1, 0)
-            mm1(c - 1, (6, 7))
-            if c % 2 == 0:
-                hc_prep(c // 2 + 1)
-            y_copy(c + 2, 0)
-            if c == last:
-                quant(c, "p_in", 512, "pq", "ps")
-                mm1(c, (0, 1, 2))
-            quant(c - 1, "r_in", 1024, "rq", "rs")
-            prod_r(c, 0)
-            if c != last:
-                quant(c, "p_in", 512, "pq", "ps")
-                if c > 0:
-                    mm1(c, (0, 1, 2))
-            mm2(c - 3)
-            prod_r(c, 1)
-            if c % 2 == 0 and c >= 2:
                 l_load(c // 2 + 2)
-            h_banks(c + 1, 1)
-            if c > 0:
-                mm1(c, (3,))
-            quant(c - 2, "q_in", 1024, "qq", "qs")
+            if c % 4 == 3 and c // 4 + 1 < NG:
+                l_load(c // 2 + 2)
+            if c in (2, 6):
+                l1_dup(c // 4 + 2, 0, GB, nc.gpsimd)
+            mm2(c - 2)
+            prod_p(c + LEAD - 1)
+            if c > 1:
+                quant(c - 1, "r_in", 1024, "rq", "rs")
+            if c % 2 == 1:
+                hc_prep(c // 2 + 1)
+            mm1(c, (0, 1, 2, 3))
+            turn_p(c + LEAD - 1, 0)
+            prod_r(c, 0)
+            h_bank(c + 1, 0)
+            mm1(c, (4, 5))
+            turn_p(c + LEAD - 1, 1)
+            quant(c - 1, "q_in", 1024, "qq", "qs")
+            prod_r(c, 1)
+            h_bank(c + 1, 1)
+            mm1(c, (6, 7))
+            quant(c + LEAD - 2, "p_in", 512, "pq", "ps")
+        mm2(last - 1)
+        quant(last, "r_in", 1024, "rq", "rs")
+        quant_q_half(last, 0)
+        mm2(last, 0, 2)
+        quant_q_half(last, 1)
+        mm2(last, 2, CB, True)

@@ -138,12 +138,12 @@ def tile_qriaffine_t_kernel(tc, layer1, layer2, layer3, h1, h2, h3, W, out):
                 nc.tensor.transpose(zb[:, n, :], z[:, n].rearrange("p x e -> p (x e)").bitcast(F32), ident_f[:])
             nc.scalar.copy(out=l0[:, CB * P * s:CB * P * (s + 1)].rearrange("p (n j) -> p n j", n=CB), in_=zb[:])
 
-        wv = W.rearrange("a b (q t) d -> q a b (t d)", t=4)
-        wraw = const.tile([P, 32, P], BF16, name="wraw")
+        wv = W.rearrange("a b (u q e) d -> q a (b u) (e d)", u=2, q=8, e=2)
+        wraw = const.tile([P, 64, 64], BF16, name="wraw")
         win = const.tile([P, 4096], BF16, name="win", align_bytes=64)
         wq = const.tile([P, 1024], U32, name="wq", align_bytes=64)
         ws = const.tile([P, 1024], U8, name="ws", align_bytes=64)
-        wr = wraw[:].rearrange("p b (t x) -> p b t x", t=4).rearrange("p (g b) t (u q e) -> p g u e b q t", g=2, u=2, e=2)
+        wr = wraw[:].rearrange("p x y -> p (x y)").rearrange("p (g b t u q e) -> p g u e b q t", g=2, b=16, t=4, u=2, q=8, e=2)
         wo = win[:].rearrange("p (g u e b q t) -> p g u e b q t", g=2, u=2, e=2, b=16, q=8, t=4)
 
         st = {}
@@ -180,7 +180,7 @@ def tile_qriaffine_t_kernel(tc, layer1, layer2, layer3, h1, h2, h3, W, out):
             for u in range(2):
                 nc.vector.tensor_tensor(
                     out=pn[:, u].rearrange("p n (a q e) -> p a n q e", a=16, e=2),
-                    in0=hw1[g][:, n0:n0 + CB].rearrange("p n (q v e) -> p n q v e", v=2, e=2)[:, :, :, u].unsqueeze(1).to_broadcast([P, 16, CB, 8, 2]),
+                    in0=hw1[g][:, n0:n0 + CB, 16 * u:16 * u + 16].rearrange("p n (q e) -> p n q e", e=2).unsqueeze(1).to_broadcast([P, 16, CB, 8, 2]),
                     in1=l1d[g][:, c % 4].unsqueeze(3).to_broadcast([P, 16, CB, 8, 2]),
                     op=MULT)
             st[c]["pn"] = pn

@@ -38,7 +38,7 @@ def tile_qriaffine_t_kernel(tc, layer1, layer2, layer3, h1, h2, h3, W, out):
         work = ctx.enter_context(tc.tile_pool(name="work", bufs=3))
         outp = ctx.enter_context(tc.tile_pool(name="outp", bufs=5))
         ps_h = ctx.enter_context(tc.psum_pool(name="ps_h", bufs=2))
-        ps_q = ctx.enter_context(tc.psum_pool(name="ps_q", bufs=3))
+        ps_q = ctx.enter_context(tc.psum_pool(name="ps_q", bufs=4))
         ctx.enter_context(tc.manual_schedule())
 
         ident_f = const.tile([P, P], F32, name="ident_f")
@@ -164,7 +164,7 @@ def tile_qriaffine_t_kernel(tc, layer1, layer2, layer3, h1, h2, h3, W, out):
         def h_bank(c, pr):
             if not ok(c):
                 return
-            hb = ps_h.tile([P, 4, 2 * P], BF16, name="hb", bufs=3)
+            hb = ps_h.tile([P, 4, 2 * P], BF16, name="hb", bufs=2)
             for i in range(4):
                 unit = 8 * (c % 2) + 4 * pr + 2 * (i % 2) + i // 2
                 nc.tensor.matmul(out=hb[:, i, :], lhsT=sel[:, unit].rearrange("p b q -> p (b q)"),
@@ -348,6 +348,7 @@ def tile_qriaffine_t_kernel(tc, layer1, layer2, layer3, h1, h2, h3, W, out):
         quant(4, "p_in", 512, "pq", "ps")
         turn_p(5, 0)
         turn_p(5, 1)
+        hc_prep(1)
 
         last = NCH - 1
         for c in range(1, NCH):
@@ -362,23 +363,23 @@ def tile_qriaffine_t_kernel(tc, layer1, layer2, layer3, h1, h2, h3, W, out):
                 l_load(c // 2 + 2)
             if c in (2, 6):
                 l1_dup(c // 4 + 2, 0, GB, nc.gpsimd)
-            mm2(c - 2)
             prod_p(c + LEAD - 1)
+            prod_r(c, 0)
+            prod_r(c, 1)
+            mm1(c, (0, 1, 2))
+            mm2(c - 2)
+            mm1(c, (3, 4, 5))
+            quant(c + LEAD - 2, "p_in", 512, "pq", "ps")
             if c > 1:
                 quant(c - 1, "r_in", 1024, "rq", "rs")
-            if c % 2 == 1:
-                hc_prep(c // 2 + 1)
-            mm1(c, (0, 1, 2, 3))
-            turn_p(c + LEAD - 1, 0)
-            prod_r(c, 0)
-            h_bank(c + 1, 0)
-            mm1(c, (4, 5))
-            turn_p(c + LEAD - 1, 1)
             quant(c - 1, "q_in", 1024, "qq", "qs")
-            prod_r(c, 1)
+            turn_p(c + LEAD - 1, 0)
+            turn_p(c + LEAD - 1, 1)
+            if c % 2 == 0:
+                hc_prep(c // 2 + 1)
+            h_bank(c + 1, 0)
             h_bank(c + 1, 1)
             mm1(c, (6, 7))
-            quant(c + LEAD - 2, "p_in", 512, "pq", "ps")
         mm2(last - 1)
         quant(last, "r_in", 1024, "rq", "rs")
         quant_q_half(last, 0)

@@ -316,34 +316,31 @@ def tile_qriaffine_t_kernel(tc, layer1, layer2, layer3, h1, h2, h3, W, out):
         h_bank(0, 1)
         quant(0, "p_in", 512, "pq", "ps")
         prod_r(0, 0)
-        w_part(0)
         prod_r(0, 1)
         quant(1, "p_in", 512, "pq", "ps")
+        w_part(0)
         w_part(1)
         l_prep(0)
         l_load(0, 4, 8)
         l_load(1)
         l1_dup(0, 8, GB, nc.vector)
-        prod_p(2)
-        quant(0, "r_in", 1024, "rq", "rs")
+        p_chunk(2)
         nc.vector.quantize_mx(out=wq[:].bitcast(FP8X4), scales=ws[:], in_=win[:])
-        turn_p(2, 0)
-        mm1(0, (0,))
-        turn_p(2, 1)
+        mm1(0, (0, 1, 2))
         prod_p(3)
-        mm1(0, (1, 2, 3))
+        quant(0, "r_in", 1024, "rq", "rs")
         turn_p(3, 0)
-        quant(2, "p_in", 512, "pq", "ps")
-        mm1(0, (4, 5))
-        h_bank(1, 0)
         turn_p(3, 1)
-        l1_dup(1, 0, GB, nc.gpsimd)
+        quant(2, "p_in", 512, "pq", "ps")
+        mm1(0, (3, 4, 5))
+        l1_dup(1, 0, GB, nc.vector)
         prod_p(4)
-        mm1(0, (6, 7))
-        quant(3, "p_in", 512, "pq", "ps")
-        turn_p(4, 0)
+        h_bank(1, 0)
         h_bank(1, 1)
+        turn_p(4, 0)
         turn_p(4, 1)
+        quant(3, "p_in", 512, "pq", "ps")
+        mm1(0, (6, 7))
         prod_p(5)
         quant(4, "p_in", 512, "pq", "ps")
         turn_p(5, 0)

@@ -50,8 +50,6 @@ def tile_qriaffine_t_kernel(tc, layer1, layer2, layer3, h1, h2, h3, W, out):
         nc.vector.tensor_copy(out=sel[:], in_=ident_b[:].rearrange("p (u q) -> p u q", u=16).unsqueeze(2).to_broadcast([P, 16, 16, 8]))
 
         lraw2 = {}
-        lraw1 = {}
-        l1d = {}
 
         def ok(c):
             return 0 <= c < NCH
@@ -61,28 +59,30 @@ def tile_qriaffine_t_kernel(tc, layer1, layer2, layer3, h1, h2, h3, W, out):
                 into[g] = inp.tile([P, GB, width], BF16, name="%s_%d" % (name, g))
             nc.sync.dma_start(out=into[g][:, lo:hi, 0:cols], in_=src.rearrange("n j w -> j n w")[:, GB * g + lo:GB * g + hi, :])
 
-        hw1 = {}
         hw2 = {}
 
-        def load_p(g, lo, hi):
-            load(lraw1, layer1, 16, 15, g, lo, hi, "lraw1")
-            load(hw1, h1, 32, 32, g, lo, hi, "hw1")
+        h1n = inp.tile([P, NUN, 8, 32], BF16, name="h1n")
+        l1n = inp.tile([P, NUN, P], BF16, name="l1n")
+        l1d = inp.tile([P, NUN, 8, 16, 2], BF16, name="l1d")
+
+        def load_p(lo, hi):
+            nc.sync.dma_start(out=l1n[:, lo:hi, 0:120],
+                              in_=layer1.rearrange("(k n) (y i) a -> (n y) k (i a)", n=UB, i=8)[:, lo:hi])
+            nc.sync.dma_start(out=h1n[:, lo:hi].rearrange("p k i w -> p k (i w)"),
+                              in_=h1.rearrange("(k n) (y i) w -> (n y) k (i w)", n=UB, i=8)[:, lo:hi])
 
         def load_r(g, lo, hi):
             load(lraw2, layer2, 32, 31, g, lo, hi, "lraw2")
             load(hw2, h2, 32, 32, g, lo, hi, "hw2")
 
-        def l1_dup(g, lo, hi, eng):
-            if g not in l1d:
-                l1d[g] = inp.tile([P, GB // CB, 16, CB, 2], BF16, name="l1d_%d" % g)
-            k0, k1 = lo // CB, hi // CB
-            eng.memset(l1d[g][:, k0:k1, 15, :, :], 1.0)
-            src = lraw1[g][:, lo:hi, 0:15].rearrange("p (k n) a -> p a k n", n=CB).unsqueeze(4).to_broadcast([P, 15, k1 - k0, CB, 2])
-            dst = l1d[g][:, k0:k1, 0:15].rearrange("p k a n e -> p a k n e")
-            if eng is nc.vector:
-                eng.tensor_copy(out=dst, in_=src)
-            else:
-                eng.tensor_scalar(out=dst, in0=src, scalar1=1.0, scalar2=0.0, op0=MULT, op1=ADD)
+        def l1_dup(lo, hi, eng):
+            eng.memset(l1d[:, lo:hi, :, 15, :], 1.0)
+            for k in range(lo, hi):
+                src = l1n[:, k, 0:120].rearrange("p (i a) -> p i a", a=15).unsqueeze(3).to_broadcast([P, 8, 15, 2])
+                if eng is nc.vector:
+                    eng.tensor_copy(out=l1d[:, k, :, 0:15], in_=src)
+                else:
+                    eng.tensor_scalar(out=l1d[:, k, :, 0:15], in0=src, scalar1=1.0, scalar2=0.0, op0=MULT, op1=ADD)
 
         flat = out.rearrange("n i j -> (n i j)")
 
@@ -93,8 +93,10 @@ def tile_qriaffine_t_kernel(tc, layer1, layer2, layer3, h1, h2, h3, W, out):
         def l_prep(g):
             lp = lpp.tile([P, 32, GB, 2], BF16, name="lp")
             nc.gpsimd.memset(lp[:, 31, :, :], 1.0)
-            nc.gpsimd.tensor_scalar(out=lp[:, 0:31, :, :], in0=lraw2[g][:, :, 0:31].rearrange("p n b -> p b n").unsqueeze(3).to_broadcast([P, 31, GB, 2]),
-                                    scalar1=1.0, scalar2=0.0, op0=MULT, op1=ADD)
+            for b0 in range(0, 32, 8):
+                b1 = min(b0 + 8, 31)
+                nc.gpsimd.tensor_scalar(out=lp[:, b0:b1, :, :], in0=lraw2[g][:, :, b0:b1].rearrange("p n b -> p b n").unsqueeze(3).to_broadcast([P, b1 - b0, GB, 2]),
+                                        scalar1=1.0, scalar2=0.0, op0=MULT, op1=ADD)
             lt = ps_q.tile([P, 4, P], F32, name="lt", tag="qb")
             for o in range(4):
                 nc.tensor.transpose(lt[:, o, :], lp[:, 8 * o:8 * o + 8].rearrange("p b n e -> p (b n e)").bitcast(F32), ident_f[:])
@@ -171,36 +173,51 @@ def tile_qriaffine_t_kernel(tc, layer1, layer2, layer3, h1, h2, h3, W, out):
                                  rhs=hcs[c // 2][:].bitcast(BF16), start=True, stop=True)
             hbs[(c, pr)] = hb
 
-        def prod_p(c):
-            if not ok(c):
-                return
-            st[c] = {}
-            g, n0 = c // 4, CB * (c % 4)
-            pn = work.tile([P, 2, CB, 256], BF16, name="pn", bufs=2)
-            for u in range(2):
-                nc.vector.tensor_tensor(
-                    out=pn[:, u].rearrange("p n (a q e) -> p a n q e", a=16, e=2),
-                    in0=hw1[g][:, n0:n0 + CB, 16 * u:16 * u + 16].rearrange("p n (q e) -> p n q e", e=2).unsqueeze(1).to_broadcast([P, 16, CB, 8, 2]),
-                    in1=l1d[g][:, c % 4].unsqueeze(3).to_broadcast([P, 16, CB, 8, 2]),
-                    op=MULT)
-            st[c]["pn"] = pn
+        pns = {}
+        p_ins = {}
+        pq = {}
 
-        def turn_p(c, pr):
-            if not ok(c):
+        def prod_p(m):
+            if not 0 <= m < 2 * NUN:
                 return
-            if pr == 0:
-                st[c]["p_in"] = work.tile([P, 2048], BF16, name="p_in", align_bytes=64, bufs=2)
-            pt = ps_h.tile([P, 2, 2, P], F32, name="pt", bufs=2)
-            for n in range(2):
+            k, i0 = m // 2, 4 * (m % 2)
+            pn = work.tile([P, 2, 4, 256], BF16, name="pn", bufs=2)
+            step = 2 if m == 0 else 4
+            for lo in range(0, 4, step):
                 for u in range(2):
-                    nc.tensor.transpose(pt[:, n, u, :], st[c]["pn"][:, u, 2 * pr + n, :].bitcast(F32), ident_f[:])
-            nc.scalar.copy(out=st[c]["p_in"][:, 1024 * pr:1024 * (pr + 1)].bitcast(F32).rearrange("p (n i u) -> p n i u", n=2, u=2),
-                           in_=pt[:].rearrange("p n u i -> p n i u"))
+                    nc.vector.tensor_tensor(
+                        out=pn[:, u, lo:lo + step].rearrange("p i (a q e) -> p i a q e", a=16, e=2),
+                        in0=h1n[:, k, i0 + lo:i0 + lo + step, 16 * u:16 * u + 16].rearrange("p i (q e) -> p i q e", e=2).unsqueeze(2).to_broadcast([P, step, 16, 8, 2]),
+                        in1=l1d[:, k, i0 + lo:i0 + lo + step].unsqueeze(3).to_broadcast([P, step, 16, 8, 2]),
+                        op=MULT)
+            pns[m] = pn
+
+        def turn_p(m, pr):
+            if not 0 <= m < 2 * NUN:
+                return
+            if m % 2 == 0 and pr == 0:
+                p_ins[m // 2] = work.tile([P, 4096], BF16, name="p_in", align_bytes=64, bufs=2)
+            pt = ps_h.tile([P, 4, P], F32, name="pt")
+            for i in range(2):
+                for u in range(2):
+                    nc.tensor.transpose(pt[:, 2 * i + u, :], pns[m][:, u, 2 * pr + i, :].bitcast(F32), ident_f[:])
+            lo = 4 * (2 * (m % 2) + pr)
+            nc.scalar.copy(out=p_ins[m // 2][:].bitcast(F32).rearrange("p (c w) -> p c w", w=16)[:, :, lo:lo + 4],
+                           in_=pt[:].rearrange("p w c -> p c w"))
+
+        def quant_p(k):
+            if not 0 <= k < NUN:
+                return
+            cd = work.tile([P, 1024], U32, name="pq", align_bytes=64, bufs=5)
+            sc = work.tile([P, 1024], U8, name="ps", align_bytes=64, bufs=5)
+            nc.vector.quantize_mx(out=cd[:].bitcast(FP8X4), scales=sc[:], in_=p_ins[k][:])
+            pq[k] = (cd, sc)
 
         def prod_r(c, pr):
             if not ok(c):
                 return
             if pr == 0:
+                st[c] = {}
                 st[c]["r_in"] = work.tile([P, 4096], BF16, name="r_in", align_bytes=64, bufs=2)
             for g in range(2):
                 lo = 1024 * (2 * pr + g)
@@ -219,31 +236,37 @@ def tile_qriaffine_t_kernel(tc, layer1, layer2, layer3, h1, h2, h3, W, out):
                 src = src[:].rearrange("p k x -> p (k x)")
             else:
                 src = src[:]
-            deep = LEAD + 2 if key == "p_in" else 3
-            cd = work.tile([P, words], U32, name=codes, align_bytes=64, bufs=deep)
-            sc = work.tile([P, words], U8, name=scales, align_bytes=64, bufs=deep)
+            cd = work.tile([P, words], U32, name=codes, align_bytes=64)
+            sc = work.tile([P, words], U8, name=scales, align_bytes=64)
             nc.vector.quantize_mx(out=cd[:].bitcast(FP8X4), scales=sc[:], in_=src)
             st[c][codes] = cd
             st[c][scales] = sc
 
-        def mm1(c, units):
+        def mm1(c, units, copy=True):
             if not ok(c):
                 return
             s = st[c]
+            pc, psc = pq[c // 2]
             if "q_in" not in s:
                 s["q_in"] = work.tile([P, 2 * CB, 512], BF16, name="q_in", align_bytes=64)
             for un in units:
                 n, g = un // 2, un % 2
+                lo = P * (CB * (c % 2) + n)
                 qb = ps_q.tile([P, 4, P], F32, name="qb")
                 for t in range(4):
                     col = (4 * g + t) * P
                     nc.tensor.matmul_mx(
                         out=qb[:, t, :],
                         lhsT=wq[:, col:col + P].bitcast(FP8X4), lhsT_scale=ws[:, col:col + P],
-                        rhs=s["pq"][:, P * n:P * (n + 1)].bitcast(FP8X4), rhs_scale=s["ps"][:, P * n:P * (n + 1)],
+                        rhs=pc[:, lo:lo + P].bitcast(FP8X4), rhs_scale=psc[:, lo:lo + P],
                         start=True, stop=True)
-                nc.scalar.copy(out=s["q_in"][:, un, :].rearrange("p (i t) -> p i t", t=4),
-                               in_=qb[:].rearrange("p t i -> p i t"))
+                s[un] = qb
+                if copy:
+                    q_copy(c, un)
+
+        def q_copy(c, un):
+            nc.scalar.copy(out=st[c]["q_in"][:, un, :].rearrange("p (i t) -> p i t", t=4),
+                           in_=st[c][un][:].rearrange("p t i -> p i t"))
 
         def quant_q_half(c, hf):
             s = st[c]
@@ -283,74 +306,68 @@ def tile_qriaffine_t_kernel(tc, layer1, layer2, layer3, h1, h2, h3, W, out):
                 nc.scalar.copy(out=osb[:, lo:hi, :], in_=ob[:, lo:hi, :])
             nc.sync.dma_start(out=out[CB * c + lo:CB * c + hi].rearrange("n i j -> i n j"), in_=osb[:, lo:hi, :])
 
-        load_p(0, 0, 4)
+        load_p(0, 1)
         load(lraw2, layer2, 32, 31, 0, 0, 8, "lraw2")
-        load_p(0, 4, 8)
         load(hw2, h2, 32, 32, 0, 0, 8, "hw2")
+        load_p(1, 3)
         for c8 in range(8):
             nc.sync.dma_start(out=wraw[c8:P:8, :, :], in_=wv[c8])
         load(lraw2, layer2, 32, 31, 0, 8, GB, "lraw2")
-        load_p(0, 8, GB)
         load(hw2, h2, 32, 32, 0, 8, GB, "hw2")
-        load_p(1, 0, GB)
         load_r(1, 0, GB)
+        load_p(3, NUN)
 
         def w_part(g):
             for u in range(2):
                 for e in range(2):
                     nc.scalar.copy(out=wo[:, g, u, e], in_=wr[:, g, u, e])
 
-        def p_chunk(c):
-            prod_p(c)
-            turn_p(c, 0)
-            turn_p(c, 1)
+        def p_half(m):
+            prod_p(m)
+            turn_p(m, 0)
+            turn_p(m, 1)
 
-        l1_dup(0, 0, 4, nc.vector)
-        p_chunk(0)
+        l1_dup(0, 1, nc.vector)
+        p_half(0)
         l_direct(0)
         l_direct(1)
-        l1_dup(0, 4, 8, nc.vector)
         hc_prep(0)
-        p_chunk(1)
+        p_half(1)
         h_bank(0, 0)
         h_bank(0, 1)
-        quant(0, "p_in", 512, "pq", "ps")
+        l1_dup(1, 3, nc.vector)
         prod_r(0, 0)
         prod_r(0, 1)
-        quant(1, "p_in", 512, "pq", "ps")
+        quant_p(0)
         w_part(0)
         w_part(1)
         l_prep(0)
         l_load(0, 4, 8)
         l_load(1)
-        l1_dup(0, 8, GB, nc.vector)
-        p_chunk(2)
-        nc.vector.quantize_mx(out=wq[:].bitcast(FP8X4), scales=ws[:], in_=win[:])
-        mm1(0, (0, 1, 2))
+        p_half(2)
         prod_p(3)
-        quant(0, "r_in", 1024, "rq", "rs")
+        nc.vector.quantize_mx(out=wq[:].bitcast(FP8X4), scales=ws[:], in_=win[:])
         turn_p(3, 0)
+        mm1(0, (0, 1, 2))
         turn_p(3, 1)
-        quant(2, "p_in", 512, "pq", "ps")
+        quant(0, "r_in", 1024, "rq", "rs")
         mm1(0, (3, 4, 5))
-        l1_dup(1, 0, GB, nc.vector)
+        for k in range(3, NUN):
+            l1_dup(k, k + 1, nc.gpsimd)
         prod_p(4)
         h_bank(1, 0)
         h_bank(1, 1)
         turn_p(4, 0)
         turn_p(4, 1)
-        quant(3, "p_in", 512, "pq", "ps")
+        quant_p(1)
         mm1(0, (6, 7))
         prod_p(5)
-        quant(4, "p_in", 512, "pq", "ps")
         turn_p(5, 0)
         turn_p(5, 1)
         hc_prep(1)
 
         last = NCH - 1
         for c in range(1, NCH):
-            if c in (1, 3):
-                load_p(c // 2 + 2, 0, GB)
             if c in (2, 6):
                 load_r(c // 4 + 2, 0, GB)
             if c % 4 == 1 and c // 4 + 1 < NG:
@@ -358,19 +375,20 @@ def tile_qriaffine_t_kernel(tc, layer1, layer2, layer3, h1, h2, h3, W, out):
                 l_load(c // 2 + 2)
             if c % 4 == 3 and c // 4 + 1 < NG:
                 l_load(c // 2 + 2)
-            if c in (2, 6):
-                l1_dup(c // 4 + 2, 0, GB, nc.gpsimd)
             prod_p(c + LEAD - 1)
             prod_r(c, 0)
             prod_r(c, 1)
             mm1(c, (0, 1, 2))
             mm2(c - 2)
-            mm1(c, (3, 4, 5))
-            quant(c + LEAD - 2, "p_in", 512, "pq", "ps")
+            mm1(c, (3, 4))
+            mm1(c, (5,), False)
+            if c % 2 == 1:
+                quant_p((c + LEAD - 2) // 2)
             if c > 1:
                 quant(c - 1, "r_in", 1024, "rq", "rs")
             quant(c - 1, "q_in", 1024, "qq", "qs")
             turn_p(c + LEAD - 1, 0)
+            q_copy(c, 5)
             turn_p(c + LEAD - 1, 1)
             if c % 2 == 0:
                 hc_prep(c // 2 + 1)

@@ -33,7 +33,7 @@ def tile_qriaffine_t_kernel(tc, layer1, layer2, layer3, h1, h2, h3, W, out):
         inp = ctx.enter_context(tc.tile_pool(name="inp", bufs=1))
         lpp = ctx.enter_context(tc.tile_pool(name="lpp", bufs=2))
         zp = ctx.enter_context(tc.tile_pool(name="zp", bufs=2))
-        hcp = ctx.enter_context(tc.tile_pool(name="hcp", bufs=3))
+        hcp = ctx.enter_context(tc.tile_pool(name="hcp", bufs=2))
         lrp = ctx.enter_context(tc.tile_pool(name="lrp", bufs=3))
         work = ctx.enter_context(tc.tile_pool(name="work", bufs=3))
         outp = ctx.enter_context(tc.tile_pool(name="outp", bufs=5))
@@ -71,9 +71,15 @@ def tile_qriaffine_t_kernel(tc, layer1, layer2, layer3, h1, h2, h3, W, out):
             nc.sync.dma_start(out=h1n[:, lo:hi].rearrange("p k i w -> p k (i w)"),
                               in_=h1.rearrange("(k n) (y i) w -> (n y) k (i w)", n=UB, i=8)[:, lo:hi])
 
+        def load_h2(g, lo, hi):
+            if g not in hw2:
+                hw2[g] = inp.tile([P, 2, GB // 2, 32], BF16, name="hw2_%d" % g)
+            for v in range(2):
+                nc.sync.dma_start(out=hw2[g][:, v, lo // 2:hi // 2, :], in_=h2[GB * g + lo + v:GB * g + hi:2].rearrange("n j w -> j n w"))
+
         def load_r(g, lo, hi):
             load(lraw2, layer2, 32, 31, g, lo, hi, "lraw2")
-            load(hw2, h2, 32, 32, g, lo, hi, "hw2")
+            load_h2(g, lo, hi)
 
         def l1_dup(lo, hi, eng):
             eng.memset(l1d[:, lo:hi, :, 15, :], 1.0)
@@ -151,26 +157,26 @@ def tile_qriaffine_t_kernel(tc, layer1, layer2, layer3, h1, h2, h3, W, out):
         st = {}
         hcs = {}
 
-        def hc_prep(o):
-            if not 0 <= o < NUN:
+        def hc_prep(g):
+            if not 0 <= g < NG:
                 return
-            g, half = o // 2, o % 2
-            hcb = ps_q.tile([P, P], F32, name="hcb", tag="qb")
-            nc.tensor.transpose(hcb[:], hw2[g][:].rearrange("p k w -> p (k w)").bitcast(F32)[:, P * half:P * (half + 1)], ident_f[:])
-            hc = hcp.tile([P, P], F32, name="hc")
+            hcb = ps_q.tile([P, 2, P], F32, name="hcb", tag="qb")
+            for v in range(2):
+                nc.tensor.transpose(hcb[:, v, :], hw2[g][:, v].rearrange("p k w -> p (k w)").bitcast(F32), ident_f[:])
+            hc = hcp.tile([P, 2, P], F32, name="hc")
             nc.scalar.copy(out=hc[:], in_=hcb[:])
-            hcs[o] = hc
+            hcs[g] = hc
 
         hbs = {}
 
         def h_bank(c, pr):
             if not ok(c):
                 return
-            hb = ps_h.tile([P, 4, 2 * P], BF16, name="hb", bufs=2)
-            for i in range(4):
-                unit = 8 * (c % 2) + 4 * pr + 2 * (i % 2) + i // 2
-                nc.tensor.matmul(out=hb[:, i, :], lhsT=sel[:, unit].rearrange("p b q -> p (b q)"),
-                                 rhs=hcs[c // 2][:].bitcast(BF16), start=True, stop=True)
+            hb = ps_h.tile([P, 2, 4 * P], BF16, name="hb")
+            for u in range(2):
+                unit = 2 * (2 * (c % 4) + pr) + u
+                nc.tensor.matmul(out=hb[:, u, :], lhsT=sel[:, unit].rearrange("p b q -> p (b q)"),
+                                 rhs=hcs[c // 4][:].rearrange("p v j -> p (v j)").bitcast(BF16), start=True, stop=True)
             hbs[(c, pr)] = hb
 
         pns = {}
@@ -268,14 +274,14 @@ def tile_qriaffine_t_kernel(tc, layer1, layer2, layer3, h1, h2, h3, W, out):
             nc.scalar.copy(out=st[c]["q_in"][:, un, :].rearrange("p (i t) -> p i t", t=4),
                            in_=st[c][un][:].rearrange("p t i -> p i t"))
 
-        def quant_q_half(c, hf):
+        def quant_q_part(c, lo, hi):
             s = st[c]
-            if hf == 0:
+            if lo == 0:
                 s["qq"] = work.tile([P, 1024], U32, name="qq", align_bytes=64)
                 s["qs"] = work.tile([P, 1024], U8, name="qs", align_bytes=64)
             nc.vector.quantize_mx(
-                out=s["qq"][:, 512 * hf:512 * (hf + 1)].bitcast(FP8X4), scales=s["qs"][:, 512 * hf:512 * (hf + 1)],
-                in_=s["q_in"][:].rearrange("p k x -> p (k x)")[:, 2048 * hf:2048 * (hf + 1)])
+                out=s["qq"][:, 256 * lo:256 * hi].bitcast(FP8X4), scales=s["qs"][:, 256 * lo:256 * hi],
+                in_=s["q_in"][:].rearrange("p k x -> p (k x)")[:, 1024 * lo:1024 * hi])
 
         def mm2(c, lo=0, hi=CB, vector=False, late=False):
             if not ok(c):
@@ -308,19 +314,21 @@ def tile_qriaffine_t_kernel(tc, layer1, layer2, layer3, h1, h2, h3, W, out):
 
         load_p(0, 1)
         load(lraw2, layer2, 32, 31, 0, 0, 8, "lraw2")
-        load(hw2, h2, 32, 32, 0, 0, 8, "hw2")
+        load_h2(0, 0, GB)
         load_p(1, 3)
         for c8 in range(8):
             nc.sync.dma_start(out=wraw[c8:P:8, :, :], in_=wv[c8])
         load(lraw2, layer2, 32, 31, 0, 8, GB, "lraw2")
-        load(hw2, h2, 32, 32, 0, 8, GB, "hw2")
         load_r(1, 0, GB)
         load_p(3, NUN)
 
         def w_part(g):
             for u in range(2):
                 for e in range(2):
-                    nc.scalar.copy(out=wo[:, g, u, e], in_=wr[:, g, u, e])
+                    if g == 1 and u == 1 and e == 1:
+                        nc.vector.tensor_copy(out=wo[:, g, u, e], in_=wr[:, g, u, e])
+                    else:
+                        nc.scalar.copy(out=wo[:, g, u, e], in_=wr[:, g, u, e])
 
         def p_half(m):
             prod_p(m)
@@ -336,6 +344,7 @@ def tile_qriaffine_t_kernel(tc, layer1, layer2, layer3, h1, h2, h3, W, out):
         h_bank(0, 0)
         h_bank(0, 1)
         l1_dup(1, 3, nc.vector)
+        prod_p(2)
         prod_r(0, 0)
         prod_r(0, 1)
         quant_p(0)
@@ -344,7 +353,8 @@ def tile_qriaffine_t_kernel(tc, layer1, layer2, layer3, h1, h2, h3, W, out):
         l_prep(0)
         l_load(0, 4, 8)
         l_load(1)
-        p_half(2)
+        turn_p(2, 0)
+        turn_p(2, 1)
         prod_p(3)
         nc.vector.quantize_mx(out=wq[:].bitcast(FP8X4), scales=ws[:], in_=win[:])
         turn_p(3, 0)
@@ -359,12 +369,11 @@ def tile_qriaffine_t_kernel(tc, layer1, layer2, layer3, h1, h2, h3, W, out):
         h_bank(1, 1)
         turn_p(4, 0)
         turn_p(4, 1)
-        quant_p(1)
         mm1(0, (6, 7))
         prod_p(5)
+        quant_p(1)
         turn_p(5, 0)
         turn_p(5, 1)
-        hc_prep(1)
 
         last = NCH - 1
         for c in range(1, NCH):
@@ -390,14 +399,16 @@ def tile_qriaffine_t_kernel(tc, layer1, layer2, layer3, h1, h2, h3, W, out):
             turn_p(c + LEAD - 1, 0)
             q_copy(c, 5)
             turn_p(c + LEAD - 1, 1)
-            if c % 2 == 0:
-                hc_prep(c // 2 + 1)
+            if c % 4 == 2:
+                hc_prep(c // 4 + 1)
             h_bank(c + 1, 0)
             h_bank(c + 1, 1)
             mm1(c, (6, 7))
         mm2(last - 1)
         quant(last, "r_in", 1024, "rq", "rs")
-        quant_q_half(last, 0)
+        quant_q_part(last, 0, 2)
         mm2(last, 0, 2)
-        quant_q_half(last, 1)
-        mm2(last, 2, CB, True)
+        quant_q_part(last, 2, 3)
+        mm2(last, 2, 3)
+        quant_q_part(last, 3, CB)
+        mm2(last, 3, CB, True)

from contextlib import ExitStack

import concourse.mybir as mybir
from concourse.masks import make_identity

F32 = mybir.dt.float32
BF16 = mybir.dt.bfloat16
U8 = mybir.dt.uint8
U32 = mybir.dt.uint32
FP8X4 = mybir.dt.float8_e4m3fn_x4
MULT = mybir.AluOpType.mult
ADD = mybir.AluOpType.add

P = 128
NB = 64
CB = 4
NCH = NB // CB
GB = 16
NG = NB // GB
UB = 8
NUN = NB // UB
LEAD = 6
FLOPS = 2 * 8192 * 512 * 1024 + 2 * 64 * 128 * 128 * 1024

LS_WORDS = 16 * GB * 2 * P
LS_BASE = NB * P * P - NG * LS_WORDS


def tile_qriaffine_t_kernel(tc, layer1, layer2, layer3, h1, h2, h3, W, out):
    nc = tc.nc
    with ExitStack() as ctx:
        const = ctx.enter_context(tc.tile_pool(name="const", bufs=1))
        inp = ctx.enter_context(tc.tile_pool(name="inp", bufs=1))
        lpp = ctx.enter_context(tc.tile_pool(name="lpp", bufs=2))
        zp = ctx.enter_context(tc.tile_pool(name="zp", bufs=2))
        hcp = ctx.enter_context(tc.tile_pool(name="hcp", bufs=2))
        lrp = ctx.enter_context(tc.tile_pool(name="lrp", bufs=3))
        work = ctx.enter_context(tc.tile_pool(name="work", bufs=3))
        outp = ctx.enter_context(tc.tile_pool(name="outp", bufs=5))
        ps_h = ctx.enter_context(tc.psum_pool(name="ps_h", bufs=2))
        ps_q = ctx.enter_context(tc.psum_pool(name="ps_q", bufs=4))
        ctx.enter_context(tc.manual_schedule())

        ident_f = const.tile([P, P], F32, name="ident_f")
        make_identity(nc, ident_f[:])
        ident_b = const.tile([P, P], BF16, name="ident_b")
        make_identity(nc, ident_b[:])

        sel = const.tile([P, 16, 16, 8], BF16, name="sel")
        nc.vector.tensor_copy(out=sel[:], in_=ident_b[:].rearrange("p (u q) -> p u q", u=16).unsqueeze(2).to_broadcast([P, 16, 16, 8]))

        lraw2 = {}

        def ok(c):
            return 0 <= c < NCH

        def load(into, src, width, cols, g, lo, hi, name):
            if g not in into:
                into[g] = inp.tile([P, GB, width], BF16, name="%s_%d" % (name, g))
            nc.sync.dma_start(out=into[g][:, lo:hi, 0:cols], in_=src.rearrange("n j w -> j n w")[:, GB * g + lo:GB * g + hi, :])

        hw2 = {}

        h1n = inp.tile([P, NUN, 8, 32], BF16, name="h1n")
        l1n = inp.tile([P, NUN, P], BF16, name="l1n")
        l1d = inp.tile([P, NUN, 8, 16, 2], BF16, name="l1d")

        def load_p(lo, hi):
            nc.sync.dma_start(out=l1n[:, lo:hi, 0:120],
                              in_=layer1.rearrange("(k n) (y i) a -> (n y) k (i a)", n=UB, i=8)[:, lo:hi])
            nc.sync.dma_start(out=h1n[:, lo:hi].rearrange("p k i w -> p k (i w)"),
                              in_=h1.rearrange("(k n) (y i) w -> (n y) k (i w)", n=UB, i=8)[:, lo:hi])

        def load_h2(g, lo, hi):
            if g not in hw2:
                hw2[g] = inp.tile([P, 2, GB // 2, 32], BF16, name="hw2_%d" % g)
            for v in range(2):
                nc.sync.dma_start(out=hw2[g][:, v, lo // 2:hi // 2, :], in_=h2[GB * g + lo + v:GB * g + hi:2].rearrange("n j w -> j n w"))

        def load_r(g, lo, hi):
            load(lraw2, layer2, 32, 31, g, lo, hi, "lraw2")
            load_h2(g, lo, hi)

        def l1_dup(lo, hi, eng):
            eng.memset(l1d[:, lo:hi, :, 15, :], 1.0)
            for k in range(lo, hi):
                src = l1n[:, k, 0:120].rearrange("p (i a) -> p i a", a=15).unsqueeze(3).to_broadcast([P, 8, 15, 2])
                if eng is nc.vector:
                    eng.tensor_copy(out=l1d[:, k, :, 0:15], in_=src)
                else:
                    eng.tensor_scalar(out=l1d[:, k, :, 0:15], in0=src, scalar1=1.0, scalar2=0.0, op0=MULT, op1=ADD)

        flat = out.rearrange("n i j -> (n i j)")

        def scratch2(g):
            lo = LS_BASE + g * LS_WORDS
            return flat[lo:lo + LS_WORDS]

        def l_prep(g):
            lp = lpp.tile([P, 32, GB, 2], BF16, name="lp")
            nc.gpsimd.memset(lp[:, 31, :, :], 1.0)
            for b0 in range(0, 32, 8):
                b1 = min(b0 + 8, 31)
                nc.gpsimd.tensor_scalar(out=lp[:, b0:b1, :, :], in0=lraw2[g][:, :, b0:b1].rearrange("p n b -> p b n").unsqueeze(3).to_broadcast([P, b1 - b0, GB, 2]),
                                        scalar1=1.0, scalar2=0.0, op0=MULT, op1=ADD)
            lt = ps_q.tile([P, 4, P], F32, name="lt", tag="qb")
            for o in range(4):
                nc.tensor.transpose(lt[:, o, :], lp[:, 8 * o:8 * o + 8].rearrange("p b n e -> p (b n e)").bitcast(F32), ident_f[:])
            lcw = lpp.tile([P, 4, P], F32, name="lcw")
            nc.scalar.copy(out=lcw[:], in_=lt[:])
            d2 = scratch2(g).rearrange("(g xh b n w) -> g (b n) xh w", xh=2, b=8, n=GB, g=2, w=P)
            for gg in range(2):
                nc.sync.dma_start(out=d2[gg], in_=lcw[:, 2 * gg:2 * gg + 2, :])

        lrep2 = {}
        l0 = const.tile([P, 2 * CB * P], F32, name="l0")

        def l2_words(c, g, n):
            if c == 0:
                return l0[:, P * (CB * g + n):P * (CB * g + n + 2)]
            n += CB * (c % 2)
            return lrep2[c // 2][:, P * (UB * g + n):P * (UB * g + n + 2)]

        def l_tiles(un):
            if un not in lrep2:
                lrep2[un] = lrp.tile([P, UB * 2 * P], F32, name="lrep2")

        def l_load(un, lo=0, hi=UB):
            if not 0 <= un < NUN:
                return
            g, half = un // 2, un % 2
            l_tiles(un)
            s2 = scratch2(g).rearrange("(g x m) -> x g m", g=2, x=16)[:, :, P * (UB * half + lo):P * (UB * half + hi)]
            for r in (0, 4, 1, 5, 2, 6, 3, 7):
                nc.sync.dma_start(out=lrep2[un][r:P:8, :].rearrange("p (g m) -> p g m", g=2)[:, :, P * lo:P * hi], in_=s2)

        def l_direct(s):
            z = zp.tile([P, CB, 16, 16], BF16, name="z")
            if s == 0:
                nc.vector.tensor_copy(out=z[:], in_=lraw2[0][:, 0:CB, 0:16].unsqueeze(3).to_broadcast([P, CB, 16, 16]))
            else:
                nc.gpsimd.memset(z[:, :, 15, :], 1.0)
                nc.vector.tensor_copy(out=z[:, :, 0:15, :], in_=lraw2[0][:, 0:CB, 16:31].unsqueeze(3).to_broadcast([P, CB, 15, 16]))
            zb = ps_q.tile([P, CB, P], F32, name="zb", tag="qb")
            for n in range(CB):
                nc.tensor.transpose(zb[:, n, :], z[:, n].rearrange("p x e -> p (x e)").bitcast(F32), ident_f[:])
            nc.scalar.copy(out=l0[:, CB * P * s:CB * P * (s + 1)].rearrange("p (n j) -> p n j", n=CB), in_=zb[:])

        wv = W.rearrange("a b (u q e) d -> q a (b u) (e d)", u=2, q=8, e=2)
        wraw = const.tile([P, 64, 64], BF16, name="wraw")
        win = const.tile([P, 4096], BF16, name="win", align_bytes=64)
        wq = const.tile([P, 1024], U32, name="wq", align_bytes=64)
        ws = const.tile([P, 1024], U8, name="ws", align_bytes=64)
        wr = wraw[:].rearrange("p x y -> p (x y)").rearrange("p (g b t u q e) -> p g u e b q t", g=2, b=16, t=4, u=2, q=8, e=2)
        wo = win[:].rearrange("p (g u e b q t) -> p g u e b q t", g=2, u=2, e=2, b=16, q=8, t=4)

        st = {}
        hcs = {}

        def hc_prep(g):
            if not 0 <= g < NG:
                return
            hcb = ps_q.tile([P, 2, P], F32, name="hcb", tag="qb")
            for v in range(2):
                nc.tensor.transpose(hcb[:, v, :], hw2[g][:, v].rearrange("p k w -> p (k w)").bitcast(F32), ident_f[:])
            hc = hcp.tile([P, 2, P], F32, name="hc")
            nc.scalar.copy(out=hc[:], in_=hcb[:])
            hcs[g] = hc

        hbs = {}

        def h_bank(c, pr):
            if not ok(c):
                return
            hb = ps_h.tile([P, 2, 4 * P], BF16, name="hb")
            for u in range(2):
                unit = 2 * (2 * (c % 4) + pr) + u
                nc.tensor.matmul(out=hb[:, u, :], lhsT=sel[:, unit].rearrange("p b q -> p (b q)"),
                                 rhs=hcs[c // 4][:].rearrange("p v j -> p (v j)").bitcast(BF16), start=True, stop=True)
            hbs[(c, pr)] = hb

        pns = {}
        p_ins = {}
        pq = {}

        def prod_p(m):
            if not 0 <= m < 2 * NUN:
                return
            k, i0 = m // 2, 4 * (m % 2)
            pn = work.tile([P, 2, 4, 256], BF16, name="pn", bufs=2)
            step = 2 if m == 0 else 4
            for lo in range(0, 4, step):
                for u in range(2):
                    nc.vector.tensor_tensor(
                        out=pn[:, u, lo:lo + step].rearrange("p i (a q e) -> p i a q e", a=16, e=2),
                        in0=h1n[:, k, i0 + lo:i0 + lo + step, 16 * u:16 * u + 16].rearrange("p i (q e) -> p i q e", e=2).unsqueeze(2).to_broadcast([P, step, 16, 8, 2]),
                        in1=l1d[:, k, i0 + lo:i0 + lo + step].unsqueeze(3).to_broadcast([P, step, 16, 8, 2]),
                        op=MULT)
            pns[m] = pn

        def turn_p(m, pr):
            if not 0 <= m < 2 * NUN:
                return
            if m % 2 == 0 and pr == 0:
                p_ins[m // 2] = work.tile([P, 4096], BF16, name="p_in", align_bytes=64, bufs=2)
            pt = ps_h.tile([P, 4, P], F32, name="pt")
            for i in range(2):
                for u in range(2):
                    nc.tensor.transpose(pt[:, 2 * i + u, :], pns[m][:, u, 2 * pr + i, :].bitcast(F32), ident_f[:])
            lo = 4 * (2 * (m % 2) + pr)
            nc.scalar.copy(out=p_ins[m // 2][:].bitcast(F32).rearrange("p (c w) -> p c w", w=16)[:, :, lo:lo + 4],
                           in_=pt[:].rearrange("p w c -> p c w"))

        def quant_p(k):
            if not 0 <= k < NUN:
                return
            cd = work.tile([P, 1024], U32, name="pq", align_bytes=64, bufs=5)
            sc = work.tile([P, 1024], U8, name="ps", align_bytes=64, bufs=5)
            nc.vector.quantize_mx(out=cd[:].bitcast(FP8X4), scales=sc[:], in_=p_ins[k][:])
            pq[k] = (cd, sc)

        def prod_r(c, pr):
            if not ok(c):
                return
            if pr == 0:
                st[c] = {}
                st[c]["r_in"] = work.tile([P, 4096], BF16, name="r_in", align_bytes=64, bufs=2)
            for g in range(2):
                lo = 1024 * (2 * pr + g)
                nc.vector.tensor_tensor(
                    out=st[c]["r_in"][:, lo:lo + 1024].rearrange("p (c u e) -> p c u e", u=2, e=2),
                    in0=hbs[(c, pr)][:].rearrange("p k x -> p (k x)").rearrange("p (u c e) -> p c u e", u=2, e=2),
                    in1=l2_words(c, g, 2 * pr).bitcast(BF16).rearrange("p (c e) -> p c e", e=2)
                    .unsqueeze(2).to_broadcast([P, 256, 2, 2]),
                    op=MULT)

        def quant(c, key, words, codes, scales):
            if not ok(c):
                return
            src = st[c][key]
            if key == "q_in":
                src = src[:].rearrange("p k x -> p (k x)")
            else:
                src = src[:]
            cd = work.tile([P, words], U32, name=codes, align_bytes=64)
            sc = work.tile([P, words], U8, name=scales, align_bytes=64)
            nc.vector.quantize_mx(out=cd[:].bitcast(FP8X4), scales=sc[:], in_=src)
            st[c][codes] = cd
            st[c][scales] = sc

        def mm1(c, units, copy=True):
            if not ok(c):
                return
            s = st[c]
            pc, psc = pq[c // 2]
            if "q_in" not in s:
                s["q_in"] = work.tile([P, 2 * CB, 512], BF16, name="q_in", align_bytes=64)
            for un in units:
                n, g = un // 2, un % 2
                lo = P * (CB * (c % 2) + n)
                qb = ps_q.tile([P, 4, P], F32, name="qb")
                for t in range(4):
                    col = (4 * g + t) * P
                    nc.tensor.matmul_mx(
                        out=qb[:, t, :],
                        lhsT=wq[:, col:col + P].bitcast(FP8X4), lhsT_scale=ws[:, col:col + P],
                        rhs=pc[:, lo:lo + P].bitcast(FP8X4), rhs_scale=psc[:, lo:lo + P],
                        start=True, stop=True)
                s[un] = qb
                if copy:
                    q_copy(c, un)

        def q_copy(c, un):
            nc.scalar.copy(out=st[c]["q_in"][:, un, :].rearrange("p (i t) -> p i t", t=4),
                           in_=st[c][un][:].rearrange("p t i -> p i t"))

        def quant_q_part(c, lo, hi):
            s = st[c]
            if lo == 0:
                s["qq"] = work.tile([P, 1024], U32, name="qq", align_bytes=64)
                s["qs"] = work.tile([P, 1024], U8, name="qs", align_bytes=64)
            nc.vector.quantize_mx(
                out=s["qq"][:, 256 * lo:256 * hi].bitcast(FP8X4), scales=s["qs"][:, 256 * lo:256 * hi],
                in_=s["q_in"][:].rearrange("p k x -> p (k x)")[:, 1024 * lo:1024 * hi])

        def mm2(c, lo=0, hi=CB, vector=False, late=False):
            if not ok(c):
                return
            s = st[c]
            ob = ps_q.tile([P, CB, P], F32, name="ob", tag="qb")
            for n in range(lo, hi):
                for g in range(2):
                    a = (2 * n + g) * P
                    b = (4 * (n // 2) + 2 * g + n % 2) * P
                    nc.tensor.matmul_mx(
                        out=ob[:, n, :],
                        lhsT=s["qq"][:, a:a + P].bitcast(FP8X4), lhsT_scale=s["qs"][:, a:a + P],
                        rhs=s["rq"][:, b:b + P].bitcast(FP8X4), rhs_scale=s["rs"][:, b:b + P],
                        start=(g == 0), stop=(g == 1))
            st[c]["ob"] = ob
            if not late:
                store(c, lo, hi, vector)

        def store(c, lo=0, hi=CB, vector=False):
            if not ok(c):
                return
            ob = st[c]["ob"]
            osb = outp.tile([P, CB, P], F32, name="osb")
            if vector:
                nc.vector.tensor_copy(out=osb[:, lo:hi, :], in_=ob[:, lo:hi, :])
            else:
                nc.scalar.copy(out=osb[:, lo:hi, :], in_=ob[:, lo:hi, :])
            nc.sync.dma_start(out=out[CB * c + lo:CB * c + hi].rearrange("n i j -> i n j"), in_=osb[:, lo:hi, :])

        load_p(0, 1)
        load(lraw2, layer2, 32, 31, 0, 0, 8, "lraw2")
        load_h2(0, 0, GB)
        load_p(1, 3)
        for c8 in range(8):
            nc.sync.dma_start(out=wraw[c8:P:8, :, :], in_=wv[c8])
        load(lraw2, layer2, 32, 31, 0, 8, GB, "lraw2")
        load_r(1, 0, GB)
        load_p(3, NUN)

        def w_part(g):
            for u in range(2):
                for e in range(2):
                    if g == 1 and u == 1 and e == 1:
                        nc.vector.tensor_copy(out=wo[:, g, u, e], in_=wr[:, g, u, e])
                    else:
                        nc.scalar.copy(out=wo[:, g, u, e], in_=wr[:, g, u, e])

        def p_half(m):
            prod_p(m)
            turn_p(m, 0)
            turn_p(m, 1)

        l1_dup(0, 1, nc.vector)
        p_half(0)
        l_direct(0)
        l_direct(1)
        hc_prep(0)
        p_half(1)
        h_bank(0, 0)
        h_bank(0, 1)
        l1_dup(1, 3, nc.vector)
        prod_p(2)
        prod_r(0, 0)
        prod_r(0, 1)
        quant_p(0)
        w_part(0)
        w_part(1)
        l_prep(0)
        l_load(0, 4, 8)
        l_load(1)
        turn_p(2, 0)
        turn_p(2, 1)
        prod_p(3)
        nc.vector.quantize_mx(out=wq[:].bitcast(FP8X4), scales=ws[:], in_=win[:])
        turn_p(3, 0)
        mm1(0, (0, 1, 2))
        turn_p(3, 1)
        quant(0, "r_in", 1024, "rq", "rs")
        mm1(0, (3, 4, 5))
        for k in range(3, NUN):
            l1_dup(k, k + 1, nc.gpsimd)
        prod_p(4)
        h_bank(1, 0)
        h_bank(1, 1)
        turn_p(4, 0)
        turn_p(4, 1)
        mm1(0, (6, 7))
        prod_p(5)
        quant_p(1)
        turn_p(5, 0)
        turn_p(5, 1)

        last = NCH - 1
        for c in range(1, NCH):
            if c in (2, 6):
                load_r(c // 4 + 2, 0, GB)
            if c % 4 == 1 and c // 4 + 1 < NG:
                l_prep(c // 4 + 1)
                l_load(c // 2 + 2)
            if c % 4 == 3 and c // 4 + 1 < NG:
                l_load(c // 2 + 2)
            prod_p(c + LEAD - 1)
            prod_r(c, 0)
            prod_r(c, 1)
            mm1(c, (0, 1, 2))
            mm2(c - 2)
            mm1(c, (3, 4))
            mm1(c, (5,), False)
            if c % 2 == 1:
                quant_p((c + LEAD - 2) // 2)
            if c > 1:
                quant(c - 1, "r_in", 1024, "rq", "rs")
            quant(c - 1, "q_in", 1024, "qq", "qs")
            turn_p(c + LEAD - 1, 0)
            q_copy(c, 5)
            turn_p(c + LEAD - 1, 1)
            if c % 4 == 2:
                hc_prep(c // 4 + 1)
            h_bank(c + 1, 0)
            h_bank(c + 1, 1)
            mm1(c, (6, 7))
        mm2(last - 1)
        quant(last, "r_in", 1024, "rq", "rs")
        quant_q_part(last, 0, 2)
        mm2(last, 0, 2)
        quant_q_part(last, 2, 3)
        mm2(last, 2, 3)
        quant_q_part(last, 3, CB)
        mm2(last, 3, CB, True)
